import numpy as np
import ml_dtypes


def mxq(x, axis, fmt="e4m3"):
    dtype, down = {"e4m3": (ml_dtypes.float8_e4m3fn, 7), "e5m2": (ml_dtypes.float8_e5m2, 14)}[fmt]
    v = np.moveaxis(np.asarray(x, np.float32).astype(ml_dtypes.bfloat16).astype(np.float64), axis, -1)
    blocks = v.reshape(v.shape[:-1] + (-1, 32))
    amax = np.abs(blocks).max(-1, keepdims=True)
    byte = np.maximum(np.where(amax > 0, np.frexp(amax)[1] - 1 + 127, 0) - down, 1)
    scale = np.exp2(byte - 127.0)
    codes = (blocks / scale).astype(np.float32).astype(dtype).astype(np.float64)
    return np.moveaxis((codes * scale).reshape(v.shape), -1, axis)


WIDE = False


def mx_kscale(k):
    if not WIDE:
        return np.ones(k)
    levels = np.array([18, -18])
    if k % 512:
        return np.exp2(np.random.permutation(np.resize(levels, k // 32))).repeat(32)
    a = np.empty((k // 512, 16))
    for p in range(k // 512):
        a[p, :8] = np.random.permutation(np.resize(levels, 8))
        for g in range(8):
            far = levels[np.abs(levels - a[p, g]) >= 10]
            a[p, g + 8] = far[np.random.randint(len(far))]
    return np.exp2(a.ravel()).repeat(32)


BF16 = ml_dtypes.bfloat16


def bf(x):
    return np.asarray(x, np.float32).astype(BF16)


def f64(x):
    return np.asarray(x).astype(np.float64)


B, S, HID, H, KV, D = 1, 512, 1024, 16, 4, 128
EPS = 1e-6
THETA = 10000.0
HALF = D // 2
JQ, JK = H * D, KV * D
J = JQ + 2 * JK


def rotate_half_back(t):
    return np.concatenate([t[..., HALF:], -t[..., :HALF]], axis=-1)


def norm_back(z, du):
    r = 1.0 / np.sqrt(np.mean(z * z, axis=-1, keepdims=True) + EPS)
    n = z * r
    return r * (du - n * np.mean(du * n, axis=-1, keepdims=True))


def setup_inputs():
    s = mx_kscale(S)
    u = np.repeat(mx_kscale(J)[:J // 4], 4)
    uq, uk, uv = u[:JQ], u[JQ:JQ + JK], u[JQ + JK:]
    c = 0.004 / np.sqrt(HID)
    inv_freq = 1.0 / THETA ** (np.arange(0, D, 2) / D)
    pos = np.random.randint(0, S) + np.arange(S)
    freqs = pos[:, None] * inv_freq[None, :]
    emb = np.concatenate([freqs, freqs], axis=-1)
    x0 = bf(np.random.standard_normal((B, S, HID)))
    wq0 = bf(np.random.standard_normal((JQ, HID)) * c)
    wk0 = bf(np.random.standard_normal((JK, HID)) * c)
    wv0 = bf(np.random.standard_normal((JK, HID)) * c)
    q_norm_w = bf(0.5 + 0.1 * np.random.standard_normal(D))
    k_norm_w = bf(0.5 + 0.1 * np.random.standard_normal(D))
    q_pre = f64(x0) @ f64(wq0).T
    k_pre = f64(x0) @ f64(wk0).T
    v_pre = f64(x0) @ f64(wv0).T

    def draw_grad(heads, scale, uu):
        g = np.random.standard_normal((B, heads, S, D)) * np.exp2(np.random.randint(-6, 1, (B, 1, S, 1))) * scale
        return bf(g / s[None, None, :, None] * uu.reshape(1, heads, 1, D))

    grad_0 = draw_grad(H, 0.125, uq)
    grad_1 = draw_grad(KV, 0.125, uk)
    grad_2 = draw_grad(KV, 0.0625, uv)
    return {"hidden_states": bf(f64(x0) * s[None, :, None]),
            "cos": bf(np.cos(emb)[None]),
            "sin": bf(np.sin(emb)[None]),
            "Wq": bf(f64(wq0) / uq[:, None]),
            "Wk": bf(f64(wk0) / uk[:, None]),
            "Wv": bf(f64(wv0) / uv[:, None]),
            "q_norm_w": q_norm_w,
            "k_norm_w": k_norm_w,
            "q_pre": np.asarray(q_pre, np.float32),
            "k_pre": np.asarray(k_pre, np.float32),
            "v_pre": np.asarray(v_pre, np.float32),
            "grad_0": grad_0, "grad_1": grad_1, "grad_2": grad_2}


def reference(hidden_states, cos, sin, Wq, Wk, Wv, q_norm_w, k_norm_w, q_pre, k_pre, v_pre, grad_0, grad_1, grad_2):
    T = B * S
    cs = f64(cos)[:, :, None, :]
    sn = f64(sin)[:, :, None, :]
    gq = f64(grad_0).transpose(0, 2, 1, 3)
    gk = f64(grad_1).transpose(0, 2, 1, 3)
    gv = f64(grad_2).transpose(0, 2, 1, 3)
    dq = (gq * cs + rotate_half_back(gq * sn)) * f64(q_norm_w)
    dk = (gk * cs + rotate_half_back(gk * sn)) * f64(k_norm_w)
    dzq = norm_back(f64(q_pre).reshape(B, S, H, D), dq).reshape(T, JQ)
    dzk = norm_back(f64(k_pre).reshape(B, S, KV, D), dk).reshape(T, JK)
    dzv = norm_back(f64(v_pre).reshape(B, S, KV, D), gv).reshape(T, JK)
    dz = np.concatenate([dzq, dzk, dzv], axis=1)
    w = np.concatenate([f64(Wq), f64(Wk), f64(Wv)], axis=0)
    x = f64(hidden_states).reshape(T, HID)
    dx = mxq(dz, 1, "e5m2") @ mxq(w, 0, "e4m3")
    dw = mxq(dz, 0, "e5m2").T @ mxq(x, 0, "e4m3")
    return dx.reshape(B, S, HID), dw[:JQ], dw[JQ:JQ + JK], dw[JQ + JK:]

@@ -1,0 +1,457 @@
+from contextlib import ExitStack
+
+import concourse.mybir as mybir
+from concourse.masks import make_identity
+
+F32 = mybir.dt.float32
+BF16 = mybir.dt.bfloat16
+U32 = mybir.dt.uint32
+U8 = mybir.dt.uint8
+E4M3X4 = mybir.dt.float8_e4m3fn_x4
+E5M2X4 = mybir.dt.float8_e5m2_x4
+ALU = mybir.AluOpType
+ACT = mybir.ActivationFunctionType
+
+P = 128
+S = 512
+HID = 1024
+D = 128
+HALF = 64
+PACK = 4
+EPS = 1e-6
+Q_HEADS = 16
+ROPE_HEADS = 20
+HEADS = 24
+GROUP = 4
+PASSES = 6
+NT = 512
+CHUNK = 256
+FLOPS = 2 * 2 * S * HEADS * D * HID
+
+SS_LEAD = 3
+EXTRA_SS_STEPS = (15, 18)
+SCALAR_CHUNK_STEPS = (6, 7, 10, 11, 14)
+W_RING = 3
+STAGE_RING = 4
+
+
+def tile_refattention_pa_v_kernel(
+    tc, hidden_states, cos, sin, Wq, Wk, Wv, q_norm_w, k_norm_w, q_pre, k_pre, v_pre,
+    grad_0, grad_1, grad_2, out_0, out_1, out_2, out_3,
+):
+    nc = tc.nc
+    with ExitStack() as ctx:
+        sb = ctx.enter_context(tc.tile_pool(name="sb", bufs=1))
+        ps = ctx.enter_context(tc.psum_pool(name="ps", bufs=1))
+        ctx.enter_context(tc.manual_schedule())
+
+        def sbt(name, shape, dtype):
+            return sb.tile(shape, dtype, name=name, align_bytes=64)
+
+        banks = [ps.tile([P, NT], F32, name="bank%d" % b) for b in range(8)]
+        gt_bank, du_banks, dw_banks, wt_bank, o_banks = banks[0], banks[1:3], banks[3:5], banks[5], banks[6:8]
+
+        ident32 = sbt("ident32", [P, P], F32)
+        ident16 = sbt("ident16", [P, P], BF16)
+        cs_raw = [sbt("cs_raw%d" % i, [P, PACK, D], BF16) for i in range(2)]
+        wrows = sbt("wrows", [P, 2, D], BF16)
+        wcol = sbt("wcol", [P, 2, 2], F32)
+        tabs = [sbt("tab%d" % i, [P, 2, S], F32) for i in range(2)]
+        x_raw = sbt("x_raw", [P, PACK, HID], BF16)
+        x_st = [sbt("x_st%d" % i, [P, NT * PACK], BF16) for i in range(2)]
+        x_codes = sbt("x_codes", [P, HID], U32)
+        x_sc = sbt("x_sc", [P, HID], U8)
+        w_raw = [sbt("w_raw%d" % i, [P, PACK, HID], BF16) for i in range(W_RING)]
+        w_st = [sbt("w_st%d" % i, [P, CHUNK * PACK], BF16) for i in range(2)]
+        w_codes = [sbt("w_codes%d" % i, [P, HID], U32) for i in range(PASSES)]
+        w_sc = [sbt("w_sc%d" % i, [P, HID], U8) for i in range(PASSES)]
+        terms = [sbt("terms%d" % i, [P, 2, S], F32) for i in range(2)]
+        u_t = [sbt("u%d" % i, [P, PACK, D], F32) for i in range(2)]
+        junk = sbt("junk", [P, PACK, D], BF16)
+        dz = [sbt("dz%d" % i, [P, PACK, GROUP * D], BF16) for i in range(2)]
+        dz_tok = [sbt("dz_tok%d" % i, [P, D * PACK], BF16) for i in range(2)]
+        tok_codes = [sbt("tok_codes%d" % i, [P, D], U32) for i in range(2)]
+        tok_sc = [sbt("tok_sc%d" % i, [P, D], U8) for i in range(2)]
+        dz_feat = sbt("dz_feat", [P, S * 2], F32)
+        feat_codes = [sbt("feat_codes%d" % i, [P, S], U32) for i in range(PASSES)]
+        feat_sc = [sbt("feat_sc%d" % i, [P, S], U8) for i in range(PASSES)]
+        stage = [sbt("stage%d" % i, [P, HID], F32) for i in range(STAGE_RING)]
+        ss = sbt("ss", [P, HEADS, PACK], F32)
+        nden = sbt("nden", [P, HEADS, PACK], F32)
+        nr2 = sbt("nr2", [P, HEADS, PACK], F32)
+        rr = sbt("rr", [P, HEADS, PACK], F32)
+        cc = sbt("cc", [P, HEADS, PACK], F32)
+
+        spans = [(0, 2), (2, 2)] + [(h0, GROUP) for h0 in range(GROUP, HEADS, GROUP)]
+        g_of = {}
+        z_of = {}
+
+        def source(h):
+            if h < Q_HEADS:
+                return 0, h
+            if h < ROPE_HEADS:
+                return 1, h - Q_HEADS
+            return 2, h - ROPE_HEADS
+
+        def load_g(span):
+            h0, n = span
+            kind, hh = source(h0)
+            src = (grad_0, grad_1, grad_2)[kind].rearrange("b h (p j) d -> p (b h) (j d)", j=PACK)
+            t = sbt("g%d" % h0, [P, n, PACK * D], BF16)
+            nc.sync.dma_start(out=t[:], in_=src[:, hh:hh + n, :])
+            for i in range(n):
+                g_of[h0 + i] = t[:, i, :]
+
+        def load_z(span):
+            h0, n = span
+            kind, hh = source(h0)
+            src = (q_pre, k_pre, v_pre)[kind].rearrange("b (p j) f -> p (b j) f", j=PACK)
+            t = sbt("z%d" % h0, [P, PACK, n * D], F32)
+            nc.sync.dma_start(out=t[:], in_=src[:, :, hh * D:(hh + n) * D])
+            for i in range(n):
+                z_of[h0 + i] = t[:, :, i * D:(i + 1) * D]
+
+        def load_w(g):
+            kind, hh = source(g * GROUP)
+            src = (Wq, Wk, Wv)[kind][hh * D:(hh + GROUP) * D, :].rearrange("(p j) c -> p j c", j=PACK)
+            nc.sync.dma_start(out=w_raw[g % W_RING][:], in_=src)
+
+        def interleave(engine, out, in_):
+            src = in_.rearrange("p j c -> p c j")
+            dst = out.rearrange("p (c j) -> p c j", j=PACK)
+            if engine == "g":
+                nc.gpsimd.tensor_scalar(out=dst, in0=src, scalar1=1.0, scalar2=0.0, op0=ALU.mult, op1=ALU.add)
+            elif engine == "s":
+                nc.scalar.copy(out=dst, in_=src)
+            else:
+                nc.vector.tensor_copy(out=dst, in_=src)
+
+        def w_interleave(c, engine):
+            g, q = divmod(c, HID // CHUNK)
+            st = w_st[0 if engine == "g" else 1]
+            interleave(engine, st[:], w_raw[g % W_RING][:, :, q * CHUNK:(q + 1) * CHUNK])
+            return (c, st)
+
+        def w_quant(job):
+            c, st = job
+            g, q = divmod(c, HID // CHUNK)
+            cols = slice(q * CHUNK, (q + 1) * CHUNK)
+            nc.vector.quantize_mx(out=w_codes[g][:, cols].bitcast(E4M3X4), scales=w_sc[g][:, cols], in_=st[:])
+
+        def transpose_g(h):
+            dst = gt_bank[:].bitcast(BF16)
+            for j in range(PACK):
+                nc.tensor.transpose(dst[:, j * P:(j + 1) * P], g_of[h][:, j * D:(j + 1) * D], ident16[:])
+
+        def rope_terms(h):
+            gt = gt_bank[:].bitcast(BF16)[:, 0:S].unsqueeze(1).to_broadcast([P, 2, S])
+            nc.vector.tensor_tensor(out=terms[h % 2][:], in0=gt, in1=tabs[source(h)[0]][:], op=ALU.mult)
+
+        def sum_terms(h):
+            halves = du_banks[h % 2][:].rearrange("p (j a b) -> p j a b", j=PACK, a=2)
+            ident = ident32[:].rearrange("p (a b) -> p a b", a=2)
+            for j in range(PACK):
+                tok = slice(j * P, (j + 1) * P)
+                nc.tensor.matmul(out=halves[:, j, :, :], lhsT=terms[h % 2][:, 0, tok], rhs=ident,
+                                 start=True, stop=False, is_transpose=True)
+                nc.tensor.matmul(out=halves[:, j, ::-1, :], lhsT=terms[h % 2][:, 1, tok], rhs=ident,
+                                 start=False, stop=True, is_transpose=True)
+
+        def du_of(h, j):
+            if h < ROPE_HEADS:
+                return du_banks[h % 2][:, j * D:(j + 1) * D]
+            return g_of[h][:, j * D:(j + 1) * D]
+
+        def dot(h, j, u):
+            nc.vector.scalar_tensor_tensor(out=u, in0=du_of(h, j), scalar=nr2[:, h, j:j + 1], in1=z_of[h][:, j, :],
+                                           op0=ALU.mult, op1=ALU.mult, accum_out=cc[:, h, j:j + 1])
+
+        def project(h, j, u):
+            nc.vector.scalar_tensor_tensor(out=u, in0=z_of[h][:, j, :], scalar=cc[:, h, j:j + 1], in1=du_of(h, j),
+                                           op0=ALU.mult, op1=ALU.add)
+
+        def round_dz(h, j, u):
+            g, hh = divmod(h, GROUP)
+            nc.scalar.activation(out=dz[g % 2][:, j, hh * D:(hh + 1) * D], in_=u, func=ACT.Copy,
+                                 scale=rr[:, h, j:j + 1])
+
+        def round_dz_tok(h):
+            dst = dz_tok[h % 2][:].rearrange("p (c j) -> p c j", j=PACK)
+            nc.gpsimd.tensor_tensor(out=dst, in0=u_t[h % 2][:].rearrange("p j c -> p c j"),
+                                    in1=rr[:, h, :].unsqueeze(1).to_broadcast([P, D, PACK]), op=ALU.mult)
+
+        def copy_dz_tok(h):
+            g, hh = divmod(h, GROUP)
+            interleave("v", dz_tok[h % 2][:], dz[g % 2][:, :, hh * D:(hh + 1) * D])
+
+        def tok_quant(h):
+            nc.vector.quantize_mx(out=tok_codes[h % 2][:].bitcast(E5M2X4), scales=tok_sc[h % 2][:],
+                                  in_=dz_tok[h % 2][:])
+
+        def dw_pair(h):
+            return [du_banks[0], wt_bank] if h == HEADS - 1 else dw_banks
+
+        def dw_matmuls(h):
+            for half in range(2):
+                cols = slice(half * NT, (half + 1) * NT)
+                nc.tensor.matmul_mx(out=dw_pair(h)[half][:], lhsT=tok_codes[h % 2][:].bitcast(E5M2X4),
+                                    lhsT_scale=tok_sc[h % 2][:], rhs=x_codes[:, cols].bitcast(E4M3X4),
+                                    rhs_scale=x_sc[:, cols], start=True, stop=True)
+
+        stores = []
+
+        def evict(src_banks, dst, vector_half):
+            st = stage[len(stores) % STAGE_RING]
+            stores.append(dst)
+            nc.scalar.copy(out=st[:, 0:NT], in_=src_banks[0][:])
+            if vector_half:
+                nc.vector.tensor_copy(out=st[:, NT:HID], in_=src_banks[1][:])
+            else:
+                nc.scalar.copy(out=st[:, NT:HID], in_=src_banks[1][:])
+            nc.sync.dma_start(out=dst, in_=st[:])
+
+        def dw_out(h, vector_half=False):
+            kind, hh = source(h)
+            evict(dw_pair(h), (out_1, out_2, out_3)[kind][hh * D:(hh + 1) * D, :], vector_half)
+
+        def square_sum(h):
+            for j in range(PACK):
+                nc.scalar.activation(out=junk[:, j, :], in_=z_of[h][:, j, :], func=ACT.Square,
+                                     accum_out=ss[:, h, j:j + 1])
+
+        def stat_den(m):
+            nc.scalar.activation(out=nden[:, 2 * m:2 * m + 2, :], in_=ss[:, 2 * m:2 * m + 2, :], func=ACT.Copy,
+                                 scale=-1.0, bias=-D * EPS)
+
+        def stat_recip(m):
+            nc.vector.reciprocal(out=nr2[:, 2 * m:2 * m + 2, :], in_=nden[:, 2 * m:2 * m + 2, :])
+
+        def stat_root(m):
+            nc.scalar.activation(out=rr[:, 2 * m:2 * m + 2, :], in_=nr2[:, 2 * m:2 * m + 2, :], func=ACT.Sqrt,
+                                 scale=-float(D))
+
+        def word_transposes(g, js):
+            dst = wt_bank[:].rearrange("p (i u t) -> p i u t", u=2, t=P)
+            for i, j in enumerate(js):
+                words = dz[g % 2][:, j, :].bitcast(F32)
+                for u in range(2):
+                    nc.tensor.transpose(dst[:, i, u, :], words[:, u::2], ident32[:])
+
+        def word_evict(js):
+            n = len(js)
+            src = wt_bank[:, 0:n * 2 * P].rearrange("p (i u t) -> p i t u", u=2, t=P)
+            dst = dz_feat[:, js[0] * 2 * P:(js[0] + n) * 2 * P].rearrange("p (i t u) -> p i t u", u=2, t=P)
+            nc.scalar.copy(out=dst, in_=src)
+
+        def feat_quant(g, js):
+            n = len(js)
+            cols = slice(js[0] * P, (js[0] + n) * P)
+            nc.vector.quantize_mx(out=feat_codes[g][:, cols].bitcast(E5M2X4), scales=feat_sc[g][:, cols],
+                                  in_=dz_feat[:, js[0] * 2 * P:(js[0] + n) * 2 * P].bitcast(BF16))
+
+        dx_bank = {(0, 0): o_banks[0], (0, 1): o_banks[1], (1, 0): gt_bank, (1, 1): du_banks[0],
+                   (2, 0): du_banks[1], (2, 1): o_banks[0], (3, 0): o_banks[1], (3, 1): gt_bank}
+
+        def dx_matmul(j, half, g):
+            tok = slice(j * P, (j + 1) * P)
+            cols = slice(half * NT, (half + 1) * NT)
+            nc.tensor.matmul_mx(out=dx_bank[(j, half)][:], lhsT=feat_codes[g][:, tok].bitcast(E5M2X4),
+                                lhsT_scale=feat_sc[g][:, tok], rhs=w_codes[g][:, cols].bitcast(E4M3X4),
+                                rhs_scale=w_sc[g][:, cols], start=(g == 0), stop=(g == PASSES - 1))
+
+        def dx_out(j):
+            dst = out_0.rearrange("b (p j) c -> p (b j) c", j=PACK)[:, j, :]
+            evict([dx_bank[(j, 0)], dx_bank[(j, 1)]], dst, True)
+
+        nc.vector.memset(wrows[:, 0, :], 0.0)
+        make_identity(nc, ident16[:])
+        make_identity(nc, ident32[:])
+        for i, tab in enumerate((cos, sin)):
+            nc.sync.dma_start(out=cs_raw[i][:], in_=tab.rearrange("b (p j) d -> p (b j) d", j=PACK))
+        for i, w in enumerate((q_norm_w, k_norm_w)):
+            nc.sync.dma_start(out=wrows[i:i + 1, 0, :], in_=w.rearrange("(o d) -> o d", o=1))
+        load_g(spans[0])
+        load_z(spans[0])
+        nc.sync.dma_start(out=x_raw[:], in_=hidden_states.rearrange("b (p j) c -> p (b j) c", j=PACK))
+        load_g(spans[1])
+        load_z(spans[1])
+        load_w(0)
+        load_z(spans[2])
+        load_g(spans[2])
+        later_loads = []
+        for g in range(1, PASSES):
+            if g + 1 < PASSES:
+                later_loads.append((load_z, spans[g + 2]))
+            later_loads.append((load_w, g))
+            if g + 1 < PASSES:
+                later_loads.append((load_g, spans[g + 2]))
+
+        nc.vector.tensor_scalar(out=wrows[:, 1, 0:HALF], in0=wrows[:, 0, HALF:D], scalar1=-1.0, scalar2=None,
+                                op0=ALU.mult)
+        nc.vector.tensor_copy(out=wrows[:, 1, HALF:D], in_=wrows[:, 0, 0:HALF])
+        for i in range(2):
+            dst = dw_banks[i][:].bitcast(BF16)
+            for j in range(PACK):
+                nc.tensor.transpose(dst[:, j * P:(j + 1) * P], cs_raw[i][:, j, :], ident16[:])
+        wt16 = wt_bank[:].bitcast(BF16)[:, 0:2 * P].rearrange("p (i t) -> p i t", i=2)
+        for i in range(2):
+            nc.tensor.transpose(wt16[:, i, :], wrows[:, i, :], ident16[:])
+        transpose_g(0)
+        nc.vector.tensor_copy(out=wcol[:], in_=wt16[:, :, 0:2])
+        cos_t = dw_banks[0][:].bitcast(BF16)[:, 0:S]
+        sin_t = dw_banks[1][:].bitcast(BF16)[:, 0:S]
+        nc.vector.tensor_scalar(out=tabs[0][:, 0, :], in0=cos_t, scalar1=wcol[:, 0, 0:1], scalar2=None, op0=ALU.mult)
+        nc.scalar.activation(out=tabs[0][:, 1, :], in_=sin_t, func=ACT.Copy, scale=wcol[:, 1, 0:1])
+        rope_terms(0)
+        transpose_g(1)
+        sum_terms(0)
+        rope_terms(1)
+        square_sum(0)
+        square_sum(1)
+        stat_den(0)
+        stat_recip(0)
+        nc.scalar.activation(out=tabs[1][:, 0, :], in_=cos_t, func=ACT.Copy, scale=wcol[:, 0, 1:2])
+        nc.scalar.activation(out=tabs[1][:, 1, :], in_=sin_t, func=ACT.Copy, scale=wcol[:, 1, 1:2])
+        interleave("g", x_st[0][:], x_raw[:, :, 0:NT])
+        interleave("s", x_st[1][:], x_raw[:, :, NT:HID])
+        square_sum(2)
+
+        next_ss = SS_LEAD
+        next_chunk = 0
+        recip_due = {}
+        root_due = {0: 0}
+        scalar_job = None
+        for s in range(ROPE_HEADS):
+            if s in root_due:
+                stat_root(root_due[s])
+            if s >= 1:
+                for j in range(PACK):
+                    round_dz(s - 1, j, u_t[(s - 1) % 2][:, j, :])
+                gpsimd_job = w_interleave(next_chunk, "g")
+                next_chunk = next_chunk + 1
+                round_dz_tok(s - 1)
+            if s + 2 < ROPE_HEADS:
+                transpose_g(s + 2)
+            if s >= 2:
+                dw_matmuls(s - 2)
+            if s >= 7 and s % GROUP == 3:
+                for half in range(2):
+                    dx_matmul(0, half, (s - 7) // GROUP)
+            if s == ROPE_HEADS - 1:
+                for g in range(4):
+                    for half in range(2):
+                        dx_matmul(1, half, g)
+            if s + 1 < ROPE_HEADS:
+                sum_terms(s + 1)
+            feat_round = None
+            if s >= GROUP and s % GROUP < 2:
+                feat_round = (0, 1) if s % GROUP == 0 else (2, 3)
+                word_transposes(s // GROUP - 1, feat_round)
+            for j in range(PACK):
+                dot(s, j, u_t[s % 2][:, j, :])
+            if s + 2 < ROPE_HEADS:
+                rope_terms(s + 2)
+            if s >= 1:
+                tok_quant(s - 1)
+            if s in recip_due:
+                stat_recip(recip_due[s])
+                root_due[s + 1] = recip_due[s]
+            if s == 1:
+                for half in range(2):
+                    cols = slice(half * NT, (half + 1) * NT)
+                    nc.vector.quantize_mx(out=x_codes[:, cols].bitcast(E4M3X4), scales=x_sc[:, cols],
+                                          in_=x_st[half][:])
+            if s >= GROUP and s % GROUP == 2:
+                feat_quant(s // GROUP - 1, (0, 1, 2, 3))
+            if scalar_job is not None:
+                w_quant(scalar_job)
+                scalar_job = None
+            if s >= 1:
+                w_quant(gpsimd_job)
+            for j in range(PACK):
+                project(s, j, u_t[s % 2][:, j, :])
+            if s < len(later_loads):
+                later_loads[s][0](later_loads[s][1])
+            if s >= 2:
+                dw_out(s - 2)
+            for rep in range(2 if s in EXTRA_SS_STEPS else 1):
+                if next_ss < HEADS:
+                    square_sum(next_ss)
+                    if next_ss % 2 == 1:
+                        stat_den(next_ss // 2)
+                        recip_due[s + 1] = next_ss // 2
+                    next_ss = next_ss + 1
+            if s in SCALAR_CHUNK_STEPS:
+                scalar_job = w_interleave(next_chunk, "s")
+                next_chunk = next_chunk + 1
+            if feat_round is not None:
+                word_evict(feat_round)
+
+        cells = []
+        col_done = []
+        row_done = []
+        for a in range(GROUP):
+            cells.extend([(ROPE_HEADS + hh, a) for hh in range(a, GROUP)])
+            col_done.append(len(cells) - 1)
+            cells.extend([(ROPE_HEADS + a, j) for j in range(a + 1, PACK)])
+            row_done.append(len(cells) - 1)
+        due = {}
+
+        def at(tick, fn, *args):
+            due.setdefault(tick, []).append((fn, args))
+
+        last = ROPE_HEADS - 1
+        kg = PASSES - 2
+        vg = PASSES - 1
+        at(0, word_transposes, kg, (0, 1))
+        at(0, word_evict, (0, 1))
+        at(0, dw_out, last - 1)
+        at(1, copy_dz_tok, last)
+        at(1, word_transposes, kg, (2, 3))
+        at(2, tok_quant, last)
+        at(2, feat_quant, kg, (0, 1))
+        at(2, word_evict, (2, 3))
+        at(2, dw_matmuls, last)
+        for j in range(2):
+            for half in range(2):
+                at(2, dx_matmul, j, half, kg)
+        at(4, feat_quant, kg, (2, 3))
+        at(4, dx_matmul, 2, 0, kg)
+        at(5, dw_out, last)
+        for a in range(GROUP):
+            t = col_done[a]
+            at(t, word_transposes, vg, (a,))
+            at(t + 1, word_evict, (a,))
+            at(t + 3, feat_quant, vg, (a,))
+            for half in range(2):
+                at(t + 3, dx_matmul, a, half, vg)
+            at(t + 5, dx_out, a)
+            t = row_done[a]
+            at(t + 1, copy_dz_tok, ROPE_HEADS + a)
+            at(t + 2, tok_quant, ROPE_HEADS + a)
+            at(t + 2, dw_matmuls, ROPE_HEADS + a)
+            at(t + 4, dw_out, ROPE_HEADS + a, a >= 2)
+        for g in range(PASSES - 1):
+            at(col_done[0] + 6 + g, dx_matmul, 2, 1, g)
+            at(col_done[0] + 6 + g, dx_matmul, 3, 0, g)
+            at(col_done[1] + 6, dx_matmul, 3, 1, g)
+
+        def cell_u(i):
+            return u_t[(i // PACK) % 2][:, i % PACK, :]
+
+        stat_root(root_due[ROPE_HEADS])
+        for j in range(PACK):
+            round_dz(last, j, u_t[last % 2][:, j, :])
+        dw_matmuls(last - 1)
+        for g in range(kg):
+            dx_matmul(2, 0, g)
+        for i in range(2):
+            dot(cells[i][0], cells[i][1], cell_u(i))
+        for tick in range(max(due) + 1):
+            if tick + 2 < len(cells):
+                dot(cells[tick + 2][0], cells[tick + 2][1], cell_u(tick + 2))
+            if tick < len(cells):
+                project(cells[tick][0], cells[tick][1], cell_u(tick))
+                round_dz(cells[tick][0], cells[tick][1], cell_u(tick))
+            for fn, args in due.get(tick, []):
+                fn(*args)

@@ -25,14 +25,16 @@ HEADS = 24
 GROUP = 4
 PASSES = 6
 NT = 512
-CHUNK = 256
+W_CHUNKS = ((0, 384), (384, 384), (768, 256))
+X_CHUNKS = ((0, 512), (512, 512))
 FLOPS = 2 * 2 * S * HEADS * D * HID
 
 SS_LEAD = 3
 EXTRA_SS_STEPS = (15, 18)
-SCALAR_CHUNK_STEPS = (6, 7, 10, 11, 14)
+VECTOR_COPY_PHASES = (0,)
+VECTOR_EVICT_STEPS = (18, 19)
 W_RING = 3
-STAGE_RING = 4
+STAGE_RING = 5
 
 
 def tile_refattention_pa_v_kernel(
@@ -58,11 +60,10 @@ def tile_refattention_pa_v_kernel(
         wcol = sbt("wcol", [P, 2, 2], F32)
         tabs = [sbt("tab%d" % i, [P, 2, S], F32) for i in range(2)]
         x_raw = sbt("x_raw", [P, PACK, HID], BF16)
-        x_st = [sbt("x_st%d" % i, [P, NT * PACK], BF16) for i in range(2)]
         x_codes = sbt("x_codes", [P, HID], U32)
         x_sc = sbt("x_sc", [P, HID], U8)
         w_raw = [sbt("w_raw%d" % i, [P, PACK, HID], BF16) for i in range(W_RING)]
-        w_st = [sbt("w_st%d" % i, [P, CHUNK * PACK], BF16) for i in range(2)]
+        op_st = sbt("op_st", [P, NT * PACK], BF16)
         w_codes = [sbt("w_codes%d" % i, [P, HID], U32) for i in range(PASSES)]
         w_sc = [sbt("w_sc%d" % i, [P, HID], U8) for i in range(PASSES)]
         terms = [sbt("terms%d" % i, [P, 2, S], F32) for i in range(2)]
@@ -126,25 +127,29 @@ def tile_refattention_pa_v_kernel(
             else:
                 nc.vector.tensor_copy(out=dst, in_=src)
 
-        def w_interleave(c, engine):
-            g, q = divmod(c, HID // CHUNK)
-            st = w_st[0 if engine == "g" else 1]
-            interleave(engine, st[:], w_raw[g % W_RING][:, :, q * CHUNK:(q + 1) * CHUNK])
-            return (c, st)
+        chunks = [(x_raw, x_codes, x_sc, c0, n) for c0, n in X_CHUNKS]
+        for g in range(PASSES):
+            chunks.extend([(w_raw[g % W_RING], w_codes[g], w_sc[g], c0, n) for c0, n in W_CHUNKS])
 
-        def w_quant(job):
-            c, st = job
-            g, q = divmod(c, HID // CHUNK)
-            cols = slice(q * CHUNK, (q + 1) * CHUNK)
-            nc.vector.quantize_mx(out=w_codes[g][:, cols].bitcast(E4M3X4), scales=w_sc[g][:, cols], in_=st[:])
+        def chunk_interleave(c):
+            raw, codes, scales, c0, n = chunks[c]
+            interleave("g", op_st[:, 0:n * PACK], raw[:, :, c0:c0 + n])
+
+        def chunk_quant(c):
+            raw, codes, scales, c0, n = chunks[c]
+            nc.vector.quantize_mx(out=codes[:, c0:c0 + n].bitcast(E4M3X4), scales=scales[:, c0:c0 + n],
+                                  in_=op_st[:, 0:n * PACK])
+
+        def gt_of(h):
+            return (o_banks[0] if h == 1 else gt_bank)[:].bitcast(BF16)
 
         def transpose_g(h):
-            dst = gt_bank[:].bitcast(BF16)
+            dst = gt_of(h)
             for j in range(PACK):
                 nc.tensor.transpose(dst[:, j * P:(j + 1) * P], g_of[h][:, j * D:(j + 1) * D], ident16[:])
 
         def rope_terms(h):
-            gt = gt_bank[:].bitcast(BF16)[:, 0:S].unsqueeze(1).to_broadcast([P, 2, S])
+            gt = gt_of(h)[:, 0:S].unsqueeze(1).to_broadcast([P, 2, S])
             nc.vector.tensor_tensor(out=terms[h % 2][:], in0=gt, in1=tabs[source(h)[0]][:], op=ALU.mult)
 
         def sum_terms(h):
@@ -175,21 +180,16 @@ def tile_refattention_pa_v_kernel(
             nc.scalar.activation(out=dz[g % 2][:, j, hh * D:(hh + 1) * D], in_=u, func=ACT.Copy,
                                  scale=rr[:, h, j:j + 1])
 
-        def round_dz_tok(h):
-            dst = dz_tok[h % 2][:].rearrange("p (c j) -> p c j", j=PACK)
-            nc.gpsimd.tensor_tensor(out=dst, in0=u_t[h % 2][:].rearrange("p j c -> p c j"),
-                                    in1=rr[:, h, :].unsqueeze(1).to_broadcast([P, D, PACK]), op=ALU.mult)
-
-        def copy_dz_tok(h):
+        def copy_dz_tok(h, engine):
             g, hh = divmod(h, GROUP)
-            interleave("v", dz_tok[h % 2][:], dz[g % 2][:, :, hh * D:(hh + 1) * D])
+            interleave(engine, dz_tok[h % 2][:], dz[g % 2][:, :, hh * D:(hh + 1) * D])
 
         def tok_quant(h):
             nc.vector.quantize_mx(out=tok_codes[h % 2][:].bitcast(E5M2X4), scales=tok_sc[h % 2][:],
                                   in_=dz_tok[h % 2][:])
 
         def dw_pair(h):
-            return [du_banks[0], wt_bank] if h == HEADS - 1 else dw_banks
+            return du_banks if h == HEADS - 1 else dw_banks
 
         def dw_matmuls(h):
             for half in range(2):
@@ -230,16 +230,19 @@ def tile_refattention_pa_v_kernel(
             nc.scalar.activation(out=rr[:, 2 * m:2 * m + 2, :], in_=nr2[:, 2 * m:2 * m + 2, :], func=ACT.Sqrt,
                                  scale=-float(D))
 
+        def word_bank(g):
+            return wt_bank if g < ROPE_HEADS // GROUP - 1 else du_banks[1]
+
         def word_transposes(g, js):
-            dst = wt_bank[:].rearrange("p (i u t) -> p i u t", u=2, t=P)
+            dst = word_bank(g)[:].rearrange("p (i u t) -> p i u t", u=2, t=P)
             for i, j in enumerate(js):
                 words = dz[g % 2][:, j, :].bitcast(F32)
                 for u in range(2):
                     nc.tensor.transpose(dst[:, i, u, :], words[:, u::2], ident32[:])
 
-        def word_evict(js):
+        def word_evict(g, js):
             n = len(js)
-            src = wt_bank[:, 0:n * 2 * P].rearrange("p (i u t) -> p i t u", u=2, t=P)
+            src = word_bank(g)[:, 0:n * 2 * P].rearrange("p (i u t) -> p i t u", u=2, t=P)
             dst = dz_feat[:, js[0] * 2 * P:(js[0] + n) * 2 * P].rearrange("p (i t u) -> p i t u", u=2, t=P)
             nc.scalar.copy(out=dst, in_=src)
 
@@ -250,7 +253,7 @@ def tile_refattention_pa_v_kernel(
                                   in_=dz_feat[:, js[0] * 2 * P:(js[0] + n) * 2 * P].bitcast(BF16))
 
         dx_bank = {(0, 0): o_banks[0], (0, 1): o_banks[1], (1, 0): gt_bank, (1, 1): du_banks[0],
-                   (2, 0): du_banks[1], (2, 1): o_banks[0], (3, 0): o_banks[1], (3, 1): gt_bank}
+                   (2, 0): wt_bank, (2, 1): o_banks[0], (3, 0): o_banks[1], (3, 1): gt_bank}
 
         def dx_matmul(j, half, g):
             tok = slice(j * P, (j + 1) * P)
@@ -259,9 +262,9 @@ def tile_refattention_pa_v_kernel(
                                 lhsT_scale=feat_sc[g][:, tok], rhs=w_codes[g][:, cols].bitcast(E4M3X4),
                                 rhs_scale=w_sc[g][:, cols], start=(g == 0), stop=(g == PASSES - 1))
 
-        def dx_out(j):
+        def dx_out(j, vector_half):
             dst = out_0.rearrange("b (p j) c -> p (b j) c", j=PACK)[:, j, :]
-            evict([dx_bank[(j, 0)], dx_bank[(j, 1)]], dst, True)
+            evict([dx_bank[(j, 0)], dx_bank[(j, 1)]], dst, vector_half)
 
         nc.vector.memset(wrows[:, 0, :], 0.0)
         make_identity(nc, ident16[:])
@@ -302,47 +305,54 @@ def tile_refattention_pa_v_kernel(
         sin_t = dw_banks[1][:].bitcast(BF16)[:, 0:S]
         nc.vector.tensor_scalar(out=tabs[0][:, 0, :], in0=cos_t, scalar1=wcol[:, 0, 0:1], scalar2=None, op0=ALU.mult)
         nc.scalar.activation(out=tabs[0][:, 1, :], in_=sin_t, func=ACT.Copy, scale=wcol[:, 1, 0:1])
-        rope_terms(0)
         transpose_g(1)
+        rope_terms(0)
         sum_terms(0)
         rope_terms(1)
         square_sum(0)
         square_sum(1)
+        nc.scalar.activation(out=tabs[1][:, 0, :], in_=cos_t, func=ACT.Copy, scale=wcol[:, 0, 1:2])
         stat_den(0)
         stat_recip(0)
-        nc.scalar.activation(out=tabs[1][:, 0, :], in_=cos_t, func=ACT.Copy, scale=wcol[:, 0, 1:2])
         nc.scalar.activation(out=tabs[1][:, 1, :], in_=sin_t, func=ACT.Copy, scale=wcol[:, 1, 1:2])
-        interleave("g", x_st[0][:], x_raw[:, :, 0:NT])
-        interleave("s", x_st[1][:], x_raw[:, :, NT:HID])
+        stat_root(0)
+        chunk_interleave(0)
         square_sum(2)
 
         next_ss = SS_LEAD
-        next_chunk = 0
+        den_due = {}
         recip_due = {}
-        root_due = {0: 0}
-        scalar_job = None
+        root_due = {}
         for s in range(ROPE_HEADS):
-            if s in root_due:
-                stat_root(root_due[s])
+            vector_copy = s % GROUP in VECTOR_COPY_PHASES
             if s >= 1:
                 for j in range(PACK):
                     round_dz(s - 1, j, u_t[(s - 1) % 2][:, j, :])
-                gpsimd_job = w_interleave(next_chunk, "g")
-                next_chunk = next_chunk + 1
-                round_dz_tok(s - 1)
+                chunk_interleave(s)
+            if s in den_due:
+                stat_den(den_due[s])
+            if s in root_due:
+                stat_root(root_due[s])
             if s + 2 < ROPE_HEADS:
                 transpose_g(s + 2)
-            if s >= 2:
-                dw_matmuls(s - 2)
+            if s >= 3:
+                dw_matmuls(s - 3)
             if s >= 7 and s % GROUP == 3:
                 for half in range(2):
                     dx_matmul(0, half, (s - 7) // GROUP)
-            if s == ROPE_HEADS - 1:
-                for g in range(4):
-                    for half in range(2):
-                        dx_matmul(1, half, g)
             if s + 1 < ROPE_HEADS:
                 sum_terms(s + 1)
+            if s == ROPE_HEADS - 2:
+                for g in range(3):
+                    dx_matmul(1, 0, g)
+                    dx_matmul(2, 0, g)
+            if s == ROPE_HEADS - 1:
+                dx_matmul(1, 0, 3)
+                dx_matmul(2, 0, 3)
+                for g in range(4):
+                    dx_matmul(1, 1, g)
+            if s in VECTOR_EVICT_STEPS:
+                dw_out(s - 3, True)
             feat_round = None
             if s >= GROUP and s % GROUP < 2:
                 feat_round = (0, 1) if s % GROUP == 0 else (2, 3)
@@ -351,41 +361,32 @@ def tile_refattention_pa_v_kernel(
                 dot(s, j, u_t[s % 2][:, j, :])
             if s + 2 < ROPE_HEADS:
                 rope_terms(s + 2)
-            if s >= 1:
-                tok_quant(s - 1)
-            if s in recip_due:
-                stat_recip(recip_due[s])
-                root_due[s + 1] = recip_due[s]
-            if s == 1:
-                for half in range(2):
-                    cols = slice(half * NT, (half + 1) * NT)
-                    nc.vector.quantize_mx(out=x_codes[:, cols].bitcast(E4M3X4), scales=x_sc[:, cols],
-                                          in_=x_st[half][:])
+            if s in den_due:
+                stat_recip(den_due[s])
+                root_due[s + 1] = den_due[s]
+            if s >= 2:
+                tok_quant(s - 2)
+            if s >= 1 and vector_copy:
+                copy_dz_tok(s - 1, "v")
             if s >= GROUP and s % GROUP == 2:
                 feat_quant(s // GROUP - 1, (0, 1, 2, 3))
-            if scalar_job is not None:
-                w_quant(scalar_job)
-                scalar_job = None
-            if s >= 1:
-                w_quant(gpsimd_job)
+            chunk_quant(s)
             for j in range(PACK):
                 project(s, j, u_t[s % 2][:, j, :])
             if s < len(later_loads):
                 later_loads[s][0](later_loads[s][1])
-            if s >= 2:
-                dw_out(s - 2)
+            if s >= 3 and s not in VECTOR_EVICT_STEPS:
+                dw_out(s - 3)
+            if s >= 1 and not vector_copy:
+                copy_dz_tok(s - 1, "s")
             for rep in range(2 if s in EXTRA_SS_STEPS else 1):
                 if next_ss < HEADS:
                     square_sum(next_ss)
                     if next_ss % 2 == 1:
-                        stat_den(next_ss // 2)
-                        recip_due[s + 1] = next_ss // 2
+                        den_due[s + 1] = next_ss // 2
                     next_ss = next_ss + 1
-            if s in SCALAR_CHUNK_STEPS:
-                scalar_job = w_interleave(next_chunk, "s")
-                next_chunk = next_chunk + 1
             if feat_round is not None:
-                word_evict(feat_round)
+                word_evict(s // GROUP - 1, feat_round)
 
         cells = []
         col_done = []
@@ -404,33 +405,35 @@ def tile_refattention_pa_v_kernel(
         kg = PASSES - 2
         vg = PASSES - 1
         at(0, word_transposes, kg, (0, 1))
-        at(0, word_evict, (0, 1))
-        at(0, dw_out, last - 1)
-        at(1, copy_dz_tok, last)
-        at(1, word_transposes, kg, (2, 3))
-        at(2, tok_quant, last)
-        at(2, feat_quant, kg, (0, 1))
-        at(2, word_evict, (2, 3))
-        at(2, dw_matmuls, last)
+        at(0, dw_matmuls, last - 1)
+        at(0, word_evict, kg, (0, 1))
+        at(0, word_transposes, kg, (2, 3))
+        at(2, copy_dz_tok, last, "v")
+        at(2, word_evict, kg, (2, 3))
+        at(3, feat_quant, kg, (0, 1))
+        at(3, tok_quant, last)
+        at(3, dw_out, last - 1, True)
         for j in range(2):
             for half in range(2):
-                at(2, dx_matmul, j, half, kg)
+                at(4, dx_matmul, j, half, kg)
+        at(3+1, dw_matmuls, last)
         at(4, feat_quant, kg, (2, 3))
-        at(4, dx_matmul, 2, 0, kg)
-        at(5, dw_out, last)
+        at(7, dx_matmul, 2, 0, kg)
+        at(6, dw_out, last, False)
         for a in range(GROUP):
             t = col_done[a]
             at(t, word_transposes, vg, (a,))
-            at(t + 1, word_evict, (a,))
-            at(t + 3, feat_quant, vg, (a,))
+            at(t + 1, word_evict, vg, (a,))
+            at(t + 4, feat_quant, vg, (a,))
             for half in range(2):
-                at(t + 3, dx_matmul, a, half, vg)
-            at(t + 5, dx_out, a)
+                at(t + 4, dx_matmul, a, half, vg)
             t = row_done[a]
-            at(t + 1, copy_dz_tok, ROPE_HEADS + a)
-            at(t + 2, tok_quant, ROPE_HEADS + a)
-            at(t + 2, dw_matmuls, ROPE_HEADS + a)
-            at(t + 4, dw_out, ROPE_HEADS + a, a >= 2)
+            at(t + 2, copy_dz_tok, ROPE_HEADS + a, "v")
+            at(t + 2+1, tok_quant, ROPE_HEADS + a)
+            at(t + 2+1, dw_matmuls, ROPE_HEADS + a)
+        for a in range(GROUP):
+            at(col_done[a] + 6, dx_out, a, a >= 0)
+            at(row_done[a] + 5, dw_out, ROPE_HEADS + a, a >= 1)
         for g in range(PASSES - 1):
             at(col_done[0] + 6 + g, dx_matmul, 2, 1, g)
             at(col_done[0] + 6 + g, dx_matmul, 3, 0, g)
@@ -439,14 +442,14 @@ def tile_refattention_pa_v_kernel(
         def cell_u(i):
             return u_t[(i // PACK) % 2][:, i % PACK, :]
 
+        dw_matmuls(last - 2)
         stat_root(root_due[ROPE_HEADS])
         for j in range(PACK):
             round_dz(last, j, u_t[last % 2][:, j, :])
-        dw_matmuls(last - 1)
-        for g in range(kg):
-            dx_matmul(2, 0, g)
         for i in range(2):
             dot(cells[i][0], cells[i][1], cell_u(i))
+        tok_quant(last - 1)
+        dw_out(last - 2, True)
         for tick in range(max(due) + 1):
             if tick + 2 < len(cells):
                 dot(cells[tick + 2][0], cells[tick + 2][1], cell_u(tick + 2))

@@ -30,9 +30,9 @@ X_CHUNKS = ((0, 512), (512, 512))
 FLOPS = 2 * 2 * S * HEADS * D * HID
 
 SS_LEAD = 3
-EXTRA_SS_STEPS = (15, 18)
-VECTOR_COPY_PHASES = (0,)
-VECTOR_EVICT_STEPS = (18, 19)
+EXTRA_SS_STEPS = (1, 2)
+VECTOR_COPY_PHASES = ()
+PLAIN_TERMS = 2
 W_RING = 3
 STAGE_RING = 5
 
@@ -45,7 +45,6 @@ def tile_refattention_pa_v_kernel(
     with ExitStack() as ctx:
         sb = ctx.enter_context(tc.tile_pool(name="sb", bufs=1))
         ps = ctx.enter_context(tc.psum_pool(name="ps", bufs=1))
-        ctx.enter_context(tc.manual_schedule())
 
         def sbt(name, shape, dtype):
             return sb.tile(shape, dtype, name=name, align_bytes=64)
@@ -63,7 +62,7 @@ def tile_refattention_pa_v_kernel(
         x_codes = sbt("x_codes", [P, HID], U32)
         x_sc = sbt("x_sc", [P, HID], U8)
         w_raw = [sbt("w_raw%d" % i, [P, PACK, HID], BF16) for i in range(W_RING)]
-        op_st = sbt("op_st", [P, NT * PACK], BF16)
+        op_st = [sbt("op_st%d" % i, [P, NT * PACK], BF16) for i in range(2)]
         w_codes = [sbt("w_codes%d" % i, [P, HID], U32) for i in range(PASSES)]
         w_sc = [sbt("w_sc%d" % i, [P, HID], U8) for i in range(PASSES)]
         terms = [sbt("terms%d" % i, [P, 2, S], F32) for i in range(2)]
@@ -122,10 +121,13 @@ def tile_refattention_pa_v_kernel(
             dst = out.rearrange("p (c j) -> p c j", j=PACK)
             if engine == "g":
                 nc.gpsimd.tensor_scalar(out=dst, in0=src, scalar1=1.0, scalar2=0.0, op0=ALU.mult, op1=ALU.add)
-            elif engine == "s":
-                nc.scalar.copy(out=dst, in_=src)
             else:
-                nc.vector.tensor_copy(out=dst, in_=src)
+                src = in_.rearrange("p j (c i) -> p c j i", i=PACK)
+                dst = out.rearrange("p (c i j) -> p c j i", i=PACK, j=PACK)
+                if engine == "s":
+                    nc.scalar.copy(out=dst, in_=src)
+                else:
+                    nc.vector.tensor_copy(out=dst, in_=src)
 
         chunks = [(x_raw, x_codes, x_sc, c0, n) for c0, n in X_CHUNKS]
         for g in range(PASSES):
@@ -133,20 +135,21 @@ def tile_refattention_pa_v_kernel(
 
         def chunk_interleave(c):
             raw, codes, scales, c0, n = chunks[c]
-            interleave("g", op_st[:, 0:n * PACK], raw[:, :, c0:c0 + n])
+            interleave("g", op_st[c % 2][:, 0:n * PACK], raw[:, :, c0:c0 + n])
 
         def chunk_quant(c):
             raw, codes, scales, c0, n = chunks[c]
             nc.vector.quantize_mx(out=codes[:, c0:c0 + n].bitcast(E4M3X4), scales=scales[:, c0:c0 + n],
-                                  in_=op_st[:, 0:n * PACK])
+                                  in_=op_st[c % 2][:, 0:n * PACK])
 
         def gt_of(h):
-            return (o_banks[0] if h == 1 else gt_bank)[:].bitcast(BF16)
+            return (o_banks[0] if h == 1 else gt_bank)[:]
 
         def transpose_g(h):
             dst = gt_of(h)
             for j in range(PACK):
-                nc.tensor.transpose(dst[:, j * P:(j + 1) * P], g_of[h][:, j * D:(j + 1) * D], ident16[:])
+                nc.tensor.matmul(out=dst[:, j * P:(j + 1) * P], lhsT=g_of[h][:, j * D:(j + 1) * D], rhs=ident16[:],
+                                 start=True, stop=True)
 
         def rope_terms(h):
             gt = gt_of(h)[:, 0:S].unsqueeze(1).to_broadcast([P, 2, S])
@@ -158,9 +161,11 @@ def tile_refattention_pa_v_kernel(
             for j in range(PACK):
                 tok = slice(j * P, (j + 1) * P)
                 nc.tensor.matmul(out=halves[:, j, :, :], lhsT=terms[h % 2][:, 0, tok], rhs=ident,
-                                 start=True, stop=False, is_transpose=True)
+                                 start=(j == 0), stop=False, is_transpose=(j >= PLAIN_TERMS))
+            for j in range(PACK):
+                tok = slice(j * P, (j + 1) * P)
                 nc.tensor.matmul(out=halves[:, j, ::-1, :], lhsT=terms[h % 2][:, 1, tok], rhs=ident,
-                                 start=False, stop=True, is_transpose=True)
+                                 start=False, stop=(j == PACK - 1), is_transpose=True)
 
         def du_of(h, j):
             if h < ROPE_HEADS:
@@ -266,127 +271,131 @@ def tile_refattention_pa_v_kernel(
             dst = out_0.rearrange("b (p j) c -> p (b j) c", j=PACK)[:, j, :]
             evict([dx_bank[(j, 0)], dx_bank[(j, 1)]], dst, vector_half)
 
-        nc.vector.memset(wrows[:, 0, :], 0.0)
-        make_identity(nc, ident16[:])
-        make_identity(nc, ident32[:])
-        for i, tab in enumerate((cos, sin)):
-            nc.sync.dma_start(out=cs_raw[i][:], in_=tab.rearrange("b (p j) d -> p (b j) d", j=PACK))
-        for i, w in enumerate((q_norm_w, k_norm_w)):
-            nc.sync.dma_start(out=wrows[i:i + 1, 0, :], in_=w.rearrange("(o d) -> o d", o=1))
-        load_g(spans[0])
-        load_z(spans[0])
-        nc.sync.dma_start(out=x_raw[:], in_=hidden_states.rearrange("b (p j) c -> p (b j) c", j=PACK))
-        load_g(spans[1])
-        load_z(spans[1])
-        load_w(0)
-        load_z(spans[2])
-        load_g(spans[2])
-        later_loads = []
-        for g in range(1, PASSES):
-            if g + 1 < PASSES:
-                later_loads.append((load_z, spans[g + 2]))
-            later_loads.append((load_w, g))
-            if g + 1 < PASSES:
-                later_loads.append((load_g, spans[g + 2]))
+        with tc.manual_schedule():
+            nc.vector.memset(wrows[:, 0, :], 0.0)
+            make_identity(nc, ident16[:])
+            make_identity(nc, ident32[:])
+            for i, (tab, w) in enumerate(((cos, q_norm_w), (sin, k_norm_w))):
+                nc.sync.dma_start(out=cs_raw[i][:], in_=tab.rearrange("b (p j) d -> p (b j) d", j=PACK))
+                nc.sync.dma_start(out=wrows[i:i + 1, 0, :], in_=w.rearrange("(o d) -> o d", o=1))
+            load_g(spans[0])
+            load_z(spans[0])
+            nc.sync.dma_start(out=x_raw[:], in_=hidden_states.rearrange("b (p j) c -> p (b j) c", j=PACK))
+            load_g(spans[1])
+            load_z(spans[1])
+            load_w(0)
+            load_z(spans[2])
+            load_g(spans[2])
+            later_loads = []
+            for g in range(1, PASSES):
+                if g + 1 < PASSES:
+                    later_loads.append((load_z, spans[g + 2]))
+                later_loads.append((load_w, g))
+                if g + 1 < PASSES:
+                    later_loads.append((load_g, spans[g + 2]))
 
-        nc.vector.tensor_scalar(out=wrows[:, 1, 0:HALF], in0=wrows[:, 0, HALF:D], scalar1=-1.0, scalar2=None,
-                                op0=ALU.mult)
-        nc.vector.tensor_copy(out=wrows[:, 1, HALF:D], in_=wrows[:, 0, 0:HALF])
-        for i in range(2):
-            dst = dw_banks[i][:].bitcast(BF16)
-            for j in range(PACK):
-                nc.tensor.transpose(dst[:, j * P:(j + 1) * P], cs_raw[i][:, j, :], ident16[:])
-        wt16 = wt_bank[:].bitcast(BF16)[:, 0:2 * P].rearrange("p (i t) -> p i t", i=2)
-        for i in range(2):
-            nc.tensor.transpose(wt16[:, i, :], wrows[:, i, :], ident16[:])
-        transpose_g(0)
-        nc.vector.tensor_copy(out=wcol[:], in_=wt16[:, :, 0:2])
-        cos_t = dw_banks[0][:].bitcast(BF16)[:, 0:S]
-        sin_t = dw_banks[1][:].bitcast(BF16)[:, 0:S]
-        nc.vector.tensor_scalar(out=tabs[0][:, 0, :], in0=cos_t, scalar1=wcol[:, 0, 0:1], scalar2=None, op0=ALU.mult)
-        nc.scalar.activation(out=tabs[0][:, 1, :], in_=sin_t, func=ACT.Copy, scale=wcol[:, 1, 0:1])
-        transpose_g(1)
-        rope_terms(0)
-        sum_terms(0)
-        rope_terms(1)
-        square_sum(0)
-        square_sum(1)
-        nc.scalar.activation(out=tabs[1][:, 0, :], in_=cos_t, func=ACT.Copy, scale=wcol[:, 0, 1:2])
-        stat_den(0)
-        stat_recip(0)
-        nc.scalar.activation(out=tabs[1][:, 1, :], in_=sin_t, func=ACT.Copy, scale=wcol[:, 1, 1:2])
-        stat_root(0)
-        chunk_interleave(0)
-        square_sum(2)
-
-        next_ss = SS_LEAD
-        den_due = {}
-        recip_due = {}
-        root_due = {}
-        for s in range(ROPE_HEADS):
-            vector_copy = s % GROUP in VECTOR_COPY_PHASES
-            if s >= 1:
+            nc.vector.tensor_scalar(out=wrows[:, 1, 0:HALF], in0=wrows[:, 0, HALF:D], scalar1=-1.0, scalar2=None,
+                                    op0=ALU.mult)
+            nc.vector.tensor_copy(out=wrows[:, 1, HALF:D], in_=wrows[:, 0, 0:HALF])
+            wt16 = wt_bank[:].bitcast(BF16)[:, 0:2 * P].rearrange("p (i t) -> p i t", i=2)
+            for i in range(2):
+                dst = dw_banks[i][:].bitcast(BF16)
                 for j in range(PACK):
-                    round_dz(s - 1, j, u_t[(s - 1) % 2][:, j, :])
-                chunk_interleave(s)
-            if s in den_due:
-                stat_den(den_due[s])
-            if s in root_due:
-                stat_root(root_due[s])
-            if s + 2 < ROPE_HEADS:
-                transpose_g(s + 2)
-            if s >= 3:
-                dw_matmuls(s - 3)
-            if s >= 7 and s % GROUP == 3:
-                for half in range(2):
-                    dx_matmul(0, half, (s - 7) // GROUP)
-            if s + 1 < ROPE_HEADS:
-                sum_terms(s + 1)
-            if s == ROPE_HEADS - 2:
-                for g in range(3):
-                    dx_matmul(1, 0, g)
-                    dx_matmul(2, 0, g)
-            if s == ROPE_HEADS - 1:
-                dx_matmul(1, 0, 3)
-                dx_matmul(2, 0, 3)
-                for g in range(4):
-                    dx_matmul(1, 1, g)
-            if s in VECTOR_EVICT_STEPS:
-                dw_out(s - 3, True)
-            feat_round = None
-            if s >= GROUP and s % GROUP < 2:
-                feat_round = (0, 1) if s % GROUP == 0 else (2, 3)
-                word_transposes(s // GROUP - 1, feat_round)
-            for j in range(PACK):
-                dot(s, j, u_t[s % 2][:, j, :])
-            if s + 2 < ROPE_HEADS:
-                rope_terms(s + 2)
-            if s in den_due:
-                stat_recip(den_due[s])
-                root_due[s + 1] = den_due[s]
-            if s >= 2:
-                tok_quant(s - 2)
-            if s >= 1 and vector_copy:
-                copy_dz_tok(s - 1, "v")
-            if s >= GROUP and s % GROUP == 2:
-                feat_quant(s // GROUP - 1, (0, 1, 2, 3))
-            chunk_quant(s)
-            for j in range(PACK):
-                project(s, j, u_t[s % 2][:, j, :])
-            if s < len(later_loads):
-                later_loads[s][0](later_loads[s][1])
-            if s >= 3 and s not in VECTOR_EVICT_STEPS:
-                dw_out(s - 3)
-            if s >= 1 and not vector_copy:
-                copy_dz_tok(s - 1, "s")
-            for rep in range(2 if s in EXTRA_SS_STEPS else 1):
-                if next_ss < HEADS:
-                    square_sum(next_ss)
-                    if next_ss % 2 == 1:
-                        den_due[s + 1] = next_ss // 2
-                    next_ss = next_ss + 1
-            if feat_round is not None:
-                word_evict(s // GROUP - 1, feat_round)
+                    nc.tensor.transpose(dst[:, j * P:(j + 1) * P], cs_raw[i][:, j, :], ident16[:])
+                if i == 0:
+                    for k in range(2):
+                        nc.tensor.transpose(wt16[:, k, :], wrows[:, k, :], ident16[:])
+            transpose_g(0)
+            nc.vector.tensor_copy(out=wcol[:], in_=wt16[:, :, 0:2])
+            cos_t = dw_banks[0][:].bitcast(BF16)[:, 0:S]
+            sin_t = dw_banks[1][:].bitcast(BF16)[:, 0:S]
+            nc.vector.tensor_scalar(out=tabs[0][:, 0, :], in0=cos_t, scalar1=wcol[:, 0, 0:1], scalar2=None, op0=ALU.mult)
+            nc.scalar.activation(out=tabs[0][:, 1, :], in_=sin_t, func=ACT.Copy, scale=wcol[:, 1, 0:1])
+            transpose_g(1)
+            rope_terms(0)
+            sum_terms(0)
+            rope_terms(1)
+            square_sum(0)
+            square_sum(1)
+            nc.scalar.activation(out=tabs[1][:, 0, :], in_=cos_t, func=ACT.Copy, scale=wcol[:, 0, 1:2])
+            stat_den(0)
+            stat_recip(0)
+            nc.scalar.activation(out=tabs[1][:, 1, :], in_=sin_t, func=ACT.Copy, scale=wcol[:, 1, 1:2])
+            stat_root(0)
+            chunk_interleave(0)
+            chunk_interleave(1)
+            square_sum(2)
+
+            next_ss = SS_LEAD
+            den_due = {}
+            recip_due = {}
+            root_due = {}
+            for s in range(ROPE_HEADS):
+                vector_copy = s % GROUP in VECTOR_COPY_PHASES
+                if s >= 1:
+                    for j in range(PACK):
+                        round_dz(s - 1, j, u_t[(s - 1) % 2][:, j, :])
+                if s >= 2:
+                    chunk_interleave(s)
+                if s in den_due:
+                    stat_den(den_due[s])
+                if s in root_due:
+                    stat_root(root_due[s])
+                if s + 2 < ROPE_HEADS:
+                    transpose_g(s + 2)
+                if s >= 3:
+                    dw_matmuls(s - 3)
+                if s >= 7 and s % GROUP == 3:
+                    for half in range(2):
+                        dx_matmul(0, half, (s - 7) // GROUP)
+                if s + 1 < ROPE_HEADS:
+                    sum_terms(s + 1)
+                if s == ROPE_HEADS - 2:
+                    for g in range(3):
+                        dx_matmul(1, 0, g)
+                        dx_matmul(2, 0, g)
+                if s == ROPE_HEADS - 1:
+                    dx_matmul(1, 0, 3)
+                    dx_matmul(2, 0, 3)
+                    for g in range(4):
+                        dx_matmul(1, 1, g)
+                feat_round = None
+                if s >= GROUP and s % GROUP < 2:
+                    feat_round = (0, 1) if s % GROUP == 0 else (2, 3)
+                    word_transposes(s // GROUP - 1, feat_round)
+                for j in range(PACK):
+                    dot(s, j, u_t[s % 2][:, j, :])
+                if s + 2 < ROPE_HEADS:
+                    rope_terms(s + 2)
+                else:
+                    dw_out(s - 3, True)
+                if s in den_due:
+                    stat_recip(den_due[s])
+                    root_due[s + 1] = den_due[s]
+                if s >= 2:
+                    tok_quant(s - 2)
+                if s >= 1 and vector_copy:
+                    copy_dz_tok(s - 1, "v")
+                if s >= GROUP and s % GROUP == 2:
+                    feat_quant(s // GROUP - 1, (0, 1, 2, 3))
+                if s >= 1:
+                    chunk_quant(s - 1)
+                for j in range(PACK):
+                    project(s, j, u_t[s % 2][:, j, :])
+                if s < len(later_loads):
+                    later_loads[s][0](later_loads[s][1])
+                if s >= 3 and s + 2 < ROPE_HEADS:
+                    dw_out(s - 3)
+                if s >= 1 and not vector_copy:
+                    copy_dz_tok(s - 1, "s")
+                for rep in range(2 if s in EXTRA_SS_STEPS else 1):
+                    if next_ss < HEADS:
+                        square_sum(next_ss)
+                        if next_ss % 2 == 1:
+                            den_due[s + 1] = next_ss // 2
+                        next_ss = next_ss + 1
+                if feat_round is not None:
+                    word_evict(s // GROUP - 1, feat_round)
 
         cells = []
         col_done = []
@@ -443,11 +452,12 @@ def tile_refattention_pa_v_kernel(
             return u_t[(i // PACK) % 2][:, i % PACK, :]
 
         dw_matmuls(last - 2)
-        stat_root(root_due[ROPE_HEADS])
         for j in range(PACK):
             round_dz(last, j, u_t[last % 2][:, j, :])
+        stat_root(root_due[ROPE_HEADS])
         for i in range(2):
             dot(cells[i][0], cells[i][1], cell_u(i))
+        chunk_quant(last)
         tok_quant(last - 1)
         dw_out(last - 2, True)
         for tick in range(max(due) + 1):

@@ -32,9 +32,8 @@ FLOPS = 2 * 2 * S * HEADS * D * HID
 SS_LEAD = 3
 EXTRA_SS_STEPS = (1, 2)
 VECTOR_COPY_PHASES = ()
-PLAIN_TERMS = 2
 W_RING = 3
-STAGE_RING = 5
+STAGE_RING = 7
 
 
 def tile_refattention_pa_v_kernel(
@@ -67,6 +66,7 @@ def tile_refattention_pa_v_kernel(
         w_sc = [sbt("w_sc%d" % i, [P, HID], U8) for i in range(PASSES)]
         terms = [sbt("terms%d" % i, [P, 2, S], F32) for i in range(2)]
         u_t = [sbt("u%d" % i, [P, PACK, D], F32) for i in range(2)]
+        prod = sbt("prod", [P, PACK, D], BF16)
         junk = sbt("junk", [P, PACK, D], BF16)
         dz = [sbt("dz%d" % i, [P, PACK, GROUP * D], BF16) for i in range(2)]
         dz_tok = [sbt("dz_tok%d" % i, [P, D * PACK], BF16) for i in range(2)]
@@ -83,6 +83,7 @@ def tile_refattention_pa_v_kernel(
         cc = sbt("cc", [P, HEADS, PACK], F32)
 
         spans = [(0, 2), (2, 2)] + [(h0, GROUP) for h0 in range(GROUP, HEADS, GROUP)]
+        span_ending = {h0 + n - 1: slice(h0, h0 + n) for h0, n in spans}
         g_of = {}
         z_of = {}
 
@@ -143,13 +144,12 @@ def tile_refattention_pa_v_kernel(
                                   in_=op_st[c % 2][:, 0:n * PACK])
 
         def gt_of(h):
-            return (o_banks[0] if h == 1 else gt_bank)[:]
+            return (o_banks[0] if h == 1 else gt_bank)[:].bitcast(BF16)
 
         def transpose_g(h):
             dst = gt_of(h)
             for j in range(PACK):
-                nc.tensor.matmul(out=dst[:, j * P:(j + 1) * P], lhsT=g_of[h][:, j * D:(j + 1) * D], rhs=ident16[:],
-                                 start=True, stop=True)
+                nc.tensor.transpose(dst[:, j * P:(j + 1) * P], g_of[h][:, j * D:(j + 1) * D], ident16[:])
 
         def rope_terms(h):
             gt = gt_of(h)[:, 0:S].unsqueeze(1).to_broadcast([P, 2, S])
@@ -161,19 +161,17 @@ def tile_refattention_pa_v_kernel(
             for j in range(PACK):
                 tok = slice(j * P, (j + 1) * P)
                 nc.tensor.matmul(out=halves[:, j, :, :], lhsT=terms[h % 2][:, 0, tok], rhs=ident,
-                                 start=(j == 0), stop=False, is_transpose=(j >= PLAIN_TERMS))
-            for j in range(PACK):
-                tok = slice(j * P, (j + 1) * P)
+                                 start=True, stop=False, is_transpose=True)
                 nc.tensor.matmul(out=halves[:, j, ::-1, :], lhsT=terms[h % 2][:, 1, tok], rhs=ident,
-                                 start=False, stop=(j == PACK - 1), is_transpose=True)
+                                 start=False, stop=True, is_transpose=True)
 
         def du_of(h, j):
             if h < ROPE_HEADS:
                 return du_banks[h % 2][:, j * D:(j + 1) * D]
             return g_of[h][:, j * D:(j + 1) * D]
 
-        def dot(h, j, u):
-            nc.vector.scalar_tensor_tensor(out=u, in0=du_of(h, j), scalar=nr2[:, h, j:j + 1], in1=z_of[h][:, j, :],
+        def dot(h, j, slot):
+            nc.vector.scalar_tensor_tensor(out=prod[:, slot, :], in0=du_of(h, j), scalar=nr2[:, h, j:j + 1], in1=z_of[h][:, j, :],
                                            op0=ALU.mult, op1=ALU.mult, accum_out=cc[:, h, j:j + 1])
 
         def project(h, j, u):
@@ -208,11 +206,11 @@ def tile_refattention_pa_v_kernel(
         def evict(src_banks, dst, vector_half):
             st = stage[len(stores) % STAGE_RING]
             stores.append(dst)
-            nc.scalar.copy(out=st[:, 0:NT], in_=src_banks[0][:])
             if vector_half:
                 nc.vector.tensor_copy(out=st[:, NT:HID], in_=src_banks[1][:])
             else:
                 nc.scalar.copy(out=st[:, NT:HID], in_=src_banks[1][:])
+            nc.scalar.copy(out=st[:, 0:NT], in_=src_banks[0][:])
             nc.sync.dma_start(out=dst, in_=st[:])
 
         def dw_out(h, vector_half=False):
@@ -220,19 +218,19 @@ def tile_refattention_pa_v_kernel(
             evict(dw_pair(h), (out_1, out_2, out_3)[kind][hh * D:(hh + 1) * D, :], vector_half)
 
         def square_sum(h):
-            for j in range(PACK):
+            for j in reversed(range(PACK)):
                 nc.scalar.activation(out=junk[:, j, :], in_=z_of[h][:, j, :], func=ACT.Square,
                                      accum_out=ss[:, h, j:j + 1])
 
         def stat_den(m):
-            nc.scalar.activation(out=nden[:, 2 * m:2 * m + 2, :], in_=ss[:, 2 * m:2 * m + 2, :], func=ACT.Copy,
+            nc.scalar.activation(out=nden[:, m, :], in_=ss[:, m, :], func=ACT.Copy,
                                  scale=-1.0, bias=-D * EPS)
 
         def stat_recip(m):
-            nc.vector.reciprocal(out=nr2[:, 2 * m:2 * m + 2, :], in_=nden[:, 2 * m:2 * m + 2, :])
+            nc.vector.reciprocal(out=nr2[:, m, :], in_=nden[:, m, :])
 
         def stat_root(m):
-            nc.scalar.activation(out=rr[:, 2 * m:2 * m + 2, :], in_=nr2[:, 2 * m:2 * m + 2, :], func=ACT.Sqrt,
+            nc.scalar.activation(out=rr[:, m, :], in_=nr2[:, m, :], func=ACT.Sqrt,
                                  scale=-float(D))
 
         def word_bank(g):
@@ -318,10 +316,10 @@ def tile_refattention_pa_v_kernel(
             square_sum(0)
             square_sum(1)
             nc.scalar.activation(out=tabs[1][:, 0, :], in_=cos_t, func=ACT.Copy, scale=wcol[:, 0, 1:2])
-            stat_den(0)
-            stat_recip(0)
+            stat_den(span_ending[1])
+            stat_recip(span_ending[1])
             nc.scalar.activation(out=tabs[1][:, 1, :], in_=sin_t, func=ACT.Copy, scale=wcol[:, 1, 1:2])
-            stat_root(0)
+            stat_root(span_ending[1])
             chunk_interleave(0)
             chunk_interleave(1)
             square_sum(2)
@@ -364,7 +362,7 @@ def tile_refattention_pa_v_kernel(
                     feat_round = (0, 1) if s % GROUP == 0 else (2, 3)
                     word_transposes(s // GROUP - 1, feat_round)
                 for j in range(PACK):
-                    dot(s, j, u_t[s % 2][:, j, :])
+                    dot(s, j, j)
                 if s + 2 < ROPE_HEADS:
                     rope_terms(s + 2)
                 else:
@@ -372,15 +370,15 @@ def tile_refattention_pa_v_kernel(
                 if s in den_due:
                     stat_recip(den_due[s])
                     root_due[s + 1] = den_due[s]
+                if s >= GROUP and s % GROUP == 2:
+                    feat_quant(s // GROUP - 1, (0, 1, 2, 3))
                 if s >= 2:
                     tok_quant(s - 2)
                 if s >= 1 and vector_copy:
                     copy_dz_tok(s - 1, "v")
-                if s >= GROUP and s % GROUP == 2:
-                    feat_quant(s // GROUP - 1, (0, 1, 2, 3))
                 if s >= 1:
                     chunk_quant(s - 1)
-                for j in range(PACK):
+                for j in reversed(range(PACK)):
                     project(s, j, u_t[s % 2][:, j, :])
                 if s < len(later_loads):
                     later_loads[s][0](later_loads[s][1])
@@ -391,80 +389,66 @@ def tile_refattention_pa_v_kernel(
                 for rep in range(2 if s in EXTRA_SS_STEPS else 1):
                     if next_ss < HEADS:
                         square_sum(next_ss)
-                        if next_ss % 2 == 1:
-                            den_due[s + 1] = next_ss // 2
+                        if next_ss in span_ending:
+                            den_due[s + 1] = span_ending[next_ss]
                         next_ss = next_ss + 1
                 if feat_round is not None:
                     word_evict(s // GROUP - 1, feat_round)
 
-        cells = []
-        col_done = []
-        row_done = []
-        for a in range(GROUP):
-            cells.extend([(ROPE_HEADS + hh, a) for hh in range(a, GROUP)])
-            col_done.append(len(cells) - 1)
-            cells.extend([(ROPE_HEADS + a, j) for j in range(a + 1, PACK)])
-            row_done.append(len(cells) - 1)
-        due = {}
-
-        def at(tick, fn, *args):
-            due.setdefault(tick, []).append((fn, args))
 
         last = ROPE_HEADS - 1
         kg = PASSES - 2
         vg = PASSES - 1
-        at(0, word_transposes, kg, (0, 1))
-        at(0, dw_matmuls, last - 1)
-        at(0, word_evict, kg, (0, 1))
-        at(0, word_transposes, kg, (2, 3))
-        at(2, copy_dz_tok, last, "v")
-        at(2, word_evict, kg, (2, 3))
-        at(3, feat_quant, kg, (0, 1))
-        at(3, tok_quant, last)
-        at(3, dw_out, last - 1, True)
-        for j in range(2):
-            for half in range(2):
-                at(4, dx_matmul, j, half, kg)
-        at(3+1, dw_matmuls, last)
-        at(4, feat_quant, kg, (2, 3))
-        at(7, dx_matmul, 2, 0, kg)
-        at(6, dw_out, last, False)
-        for a in range(GROUP):
-            t = col_done[a]
-            at(t, word_transposes, vg, (a,))
-            at(t + 1, word_evict, vg, (a,))
-            at(t + 4, feat_quant, vg, (a,))
-            for half in range(2):
-                at(t + 4, dx_matmul, a, half, vg)
-            t = row_done[a]
-            at(t + 2, copy_dz_tok, ROPE_HEADS + a, "v")
-            at(t + 2+1, tok_quant, ROPE_HEADS + a)
-            at(t + 2+1, dw_matmuls, ROPE_HEADS + a)
-        for a in range(GROUP):
-            at(col_done[a] + 6, dx_out, a, a >= 0)
-            at(row_done[a] + 5, dw_out, ROPE_HEADS + a, a >= 1)
-        for g in range(PASSES - 1):
-            at(col_done[0] + 6 + g, dx_matmul, 2, 1, g)
-            at(col_done[0] + 6 + g, dx_matmul, 3, 0, g)
-            at(col_done[1] + 6, dx_matmul, 3, 1, g)
 
-        def cell_u(i):
-            return u_t[(i // PACK) % 2][:, i % PACK, :]
+        def cells(batch, u):
+            for i, (h, j) in enumerate(batch):
+                dot(h, j, i)
+            for i, (h, j) in reversed(list(enumerate(batch))):
+                project(h, j, u[:, i, :])
+            for i, (h, j) in enumerate(batch):
+                round_dz(h, j, u[:, i, :])
+
+        def feature_road(g, js):
+            word_transposes(g, js)
+            word_evict(g, js)
+            feat_quant(g, js)
+
+        def token_road(h, vector_half):
+            copy_dz_tok(h, "v")
+            tok_quant(h)
+            dw_matmuls(h)
+            dw_out(h, vector_half)
 
         dw_matmuls(last - 2)
+        stat_root(root_due[ROPE_HEADS])
         for j in range(PACK):
             round_dz(last, j, u_t[last % 2][:, j, :])
-        stat_root(root_due[ROPE_HEADS])
-        for i in range(2):
-            dot(cells[i][0], cells[i][1], cell_u(i))
-        chunk_quant(last)
-        tok_quant(last - 1)
-        dw_out(last - 2, True)
-        for tick in range(max(due) + 1):
-            if tick + 2 < len(cells):
-                dot(cells[tick + 2][0], cells[tick + 2][1], cell_u(tick + 2))
-            if tick < len(cells):
-                project(cells[tick][0], cells[tick][1], cell_u(tick))
-                round_dz(cells[tick][0], cells[tick][1], cell_u(tick))
-            for fn, args in due.get(tick, []):
-                fn(*args)
+        dw_out(last - 2, False)
+        feature_road(kg, (0, 1))
+        for j in range(2):
+            for half in range(2):
+                dx_matmul(j, half, kg)
+        for a in range(GROUP):
+            cells([(ROPE_HEADS + hh, a) for hh in range(a, GROUP)], u_t[0])
+            if a == 0:
+                chunk_quant(last)
+                tok_quant(last - 1)
+                dw_matmuls(last - 1)
+                dw_out(last - 1, False)
+            feature_road(vg, (a,))
+            for half in range(2):
+                dx_matmul(a, half, vg)
+            dx_out(a, a >= 0)
+            if a == 0:
+                token_road(last, False)
+                for g in range(vg):
+                    if g == kg:
+                        feature_road(kg, (2, 3))
+                        dx_matmul(2, 0, kg)
+                    dx_matmul(2, 1, g)
+                    dx_matmul(3, 0, g)
+            if a == 1:
+                for g in range(vg):
+                    dx_matmul(3, 1, g)
+            cells([(ROPE_HEADS + a, j) for j in range(a + 1, PACK)], u_t[1])
+            token_road(ROPE_HEADS + a, a >= 1)

@@ -16,24 +16,27 @@ P = 128
 S = 512
 HID = 1024
 D = 128
-HALF = 64
+HALF = D // 2
 PACK = 4
 EPS = 1e-6
 Q_HEADS = 16
 ROPE_HEADS = 20
 HEADS = 24
 GROUP = 4
-PASSES = 6
+PASSES = HEADS // GROUP
+K_PASS = PASSES - 2
+V_PASS = PASSES - 1
 NT = 512
-W_CHUNKS = ((0, 384), (384, 384), (768, 256))
-X_CHUNKS = ((0, 512), (512, 512))
 FLOPS = 2 * 2 * S * HEADS * D * HID
 
-SS_LEAD = 3
-EXTRA_SS_STEPS = (1, 2)
-VECTOR_COPY_PHASES = ()
-W_RING = 3
-STAGE_RING = 7
+X_RANGES = ((0, 512), (512, 512))
+W_RANGES = ((0, 384), (384, 384), (768, 256))
+W_BUFFERS = 3
+OUT_BUFFERS = 7
+SQUARES_AHEAD = 3
+DOUBLE_SQUARE_STEPS = (1, 2)
+DW_LAG = 3
+DX_FIRST_STEP = 7
 
 
 def tile_refattention_pa_v_kernel(
@@ -49,38 +52,40 @@ def tile_refattention_pa_v_kernel(
             return sb.tile(shape, dtype, name=name, align_bytes=64)
 
         banks = [ps.tile([P, NT], F32, name="bank%d" % b) for b in range(8)]
-        gt_bank, du_banks, dw_banks, wt_bank, o_banks = banks[0], banks[1:3], banks[3:5], banks[5], banks[6:8]
+        gt_bank, du_banks, dw_banks, word_bank, dx_banks = banks[0], banks[1:3], banks[3:5], banks[5], banks[6:8]
+        dx_bank_of = {(0, 0): dx_banks[0], (0, 1): dx_banks[1], (1, 0): gt_bank, (1, 1): du_banks[0],
+                      (2, 0): word_bank, (2, 1): dx_banks[0], (3, 0): dx_banks[1], (3, 1): gt_bank}
 
         ident32 = sbt("ident32", [P, P], F32)
         ident16 = sbt("ident16", [P, P], BF16)
-        cs_raw = [sbt("cs_raw%d" % i, [P, PACK, D], BF16) for i in range(2)]
-        wrows = sbt("wrows", [P, 2, D], BF16)
-        wcol = sbt("wcol", [P, 2, 2], F32)
-        tabs = [sbt("tab%d" % i, [P, 2, S], F32) for i in range(2)]
+        trig_raw = [sbt("trig_raw%d" % i, [P, PACK, D], BF16) for i in range(2)]
+        gain_rows = sbt("gain_rows", [P, 2, D], BF16)
+        gain_cols = sbt("gain_cols", [P, 2, 2], F32)
+        tables = [sbt("table%d" % i, [P, 2, S], F32) for i in range(2)]
         x_raw = sbt("x_raw", [P, PACK, HID], BF16)
         x_codes = sbt("x_codes", [P, HID], U32)
-        x_sc = sbt("x_sc", [P, HID], U8)
-        w_raw = [sbt("w_raw%d" % i, [P, PACK, HID], BF16) for i in range(W_RING)]
-        op_st = [sbt("op_st%d" % i, [P, NT * PACK], BF16) for i in range(2)]
+        x_scales = sbt("x_scales", [P, HID], U8)
+        w_raw = [sbt("w_raw%d" % i, [P, PACK, HID], BF16) for i in range(W_BUFFERS)]
+        side_by_side = [sbt("side_by_side%d" % i, [P, NT * PACK], BF16) for i in range(2)]
         w_codes = [sbt("w_codes%d" % i, [P, HID], U32) for i in range(PASSES)]
-        w_sc = [sbt("w_sc%d" % i, [P, HID], U8) for i in range(PASSES)]
+        w_scales = [sbt("w_scales%d" % i, [P, HID], U8) for i in range(PASSES)]
         terms = [sbt("terms%d" % i, [P, 2, S], F32) for i in range(2)]
-        u_t = [sbt("u%d" % i, [P, PACK, D], F32) for i in range(2)]
-        prod = sbt("prod", [P, PACK, D], BF16)
-        junk = sbt("junk", [P, PACK, D], BF16)
+        unscaled = [sbt("unscaled%d" % i, [P, PACK, D], F32) for i in range(2)]
+        products = sbt("products", [P, PACK, D], BF16)
+        squares = sbt("squares", [P, PACK, D], BF16)
         dz = [sbt("dz%d" % i, [P, PACK, GROUP * D], BF16) for i in range(2)]
         dz_tok = [sbt("dz_tok%d" % i, [P, D * PACK], BF16) for i in range(2)]
         tok_codes = [sbt("tok_codes%d" % i, [P, D], U32) for i in range(2)]
-        tok_sc = [sbt("tok_sc%d" % i, [P, D], U8) for i in range(2)]
+        tok_scales = [sbt("tok_scales%d" % i, [P, D], U8) for i in range(2)]
         dz_feat = sbt("dz_feat", [P, S * 2], F32)
         feat_codes = [sbt("feat_codes%d" % i, [P, S], U32) for i in range(PASSES)]
-        feat_sc = [sbt("feat_sc%d" % i, [P, S], U8) for i in range(PASSES)]
-        stage = [sbt("stage%d" % i, [P, HID], F32) for i in range(STAGE_RING)]
-        ss = sbt("ss", [P, HEADS, PACK], F32)
-        nden = sbt("nden", [P, HEADS, PACK], F32)
-        nr2 = sbt("nr2", [P, HEADS, PACK], F32)
-        rr = sbt("rr", [P, HEADS, PACK], F32)
-        cc = sbt("cc", [P, HEADS, PACK], F32)
+        feat_scales = [sbt("feat_scales%d" % i, [P, S], U8) for i in range(PASSES)]
+        results = [sbt("result%d" % i, [P, HID], F32) for i in range(OUT_BUFFERS)]
+        sum_sq = sbt("sum_sq", [P, HEADS, PACK], F32)
+        neg_den = sbt("neg_den", [P, HEADS, PACK], F32)
+        n_stat = sbt("n_stat", [P, HEADS, PACK], F32)
+        r_stat = sbt("r_stat", [P, HEADS, PACK], F32)
+        c_stat = sbt("c_stat", [P, HEADS, PACK], F32)
 
         spans = [(0, 2), (2, 2)] + [(h0, GROUP) for h0 in range(GROUP, HEADS, GROUP)]
         span_ending = {h0 + n - 1: slice(h0, h0 + n) for h0, n in spans}
@@ -98,64 +103,52 @@ def tile_refattention_pa_v_kernel(
             h0, n = span
             kind, hh = source(h0)
             src = (grad_0, grad_1, grad_2)[kind].rearrange("b h (p j) d -> p (b h) (j d)", j=PACK)
-            t = sbt("g%d" % h0, [P, n, PACK * D], BF16)
-            nc.sync.dma_start(out=t[:], in_=src[:, hh:hh + n, :])
+            loaded = sbt("g%d" % h0, [P, n, PACK * D], BF16)
+            nc.sync.dma_start(out=loaded[:], in_=src[:, hh:hh + n, :])
             for i in range(n):
-                g_of[h0 + i] = t[:, i, :]
+                g_of[h0 + i] = loaded[:, i, :]
 
         def load_z(span):
             h0, n = span
             kind, hh = source(h0)
             src = (q_pre, k_pre, v_pre)[kind].rearrange("b (p j) f -> p (b j) f", j=PACK)
-            t = sbt("z%d" % h0, [P, PACK, n * D], F32)
-            nc.sync.dma_start(out=t[:], in_=src[:, :, hh * D:(hh + n) * D])
+            loaded = sbt("z%d" % h0, [P, PACK, n * D], F32)
+            nc.sync.dma_start(out=loaded[:], in_=src[:, :, hh * D:(hh + n) * D])
             for i in range(n):
-                z_of[h0 + i] = t[:, :, i * D:(i + 1) * D]
+                z_of[h0 + i] = loaded[:, :, i * D:(i + 1) * D]
 
         def load_w(g):
             kind, hh = source(g * GROUP)
             src = (Wq, Wk, Wv)[kind][hh * D:(hh + GROUP) * D, :].rearrange("(p j) c -> p j c", j=PACK)
-            nc.sync.dma_start(out=w_raw[g % W_RING][:], in_=src)
+            nc.sync.dma_start(out=w_raw[g % W_BUFFERS][:], in_=src)
 
-        def interleave(engine, out, in_):
-            src = in_.rearrange("p j c -> p c j")
-            dst = out.rearrange("p (c j) -> p c j", j=PACK)
-            if engine == "g":
-                nc.gpsimd.tensor_scalar(out=dst, in0=src, scalar1=1.0, scalar2=0.0, op0=ALU.mult, op1=ALU.add)
-            else:
-                src = in_.rearrange("p j (c i) -> p c j i", i=PACK)
-                dst = out.rearrange("p (c i j) -> p c j i", i=PACK, j=PACK)
-                if engine == "s":
-                    nc.scalar.copy(out=dst, in_=src)
-                else:
-                    nc.vector.tensor_copy(out=dst, in_=src)
-
-        chunks = [(x_raw, x_codes, x_sc, c0, n) for c0, n in X_CHUNKS]
+        ranges = [(x_raw, x_codes, x_scales, c0, n) for c0, n in X_RANGES]
         for g in range(PASSES):
-            chunks.extend([(w_raw[g % W_RING], w_codes[g], w_sc[g], c0, n) for c0, n in W_CHUNKS])
+            ranges.extend([(w_raw[g % W_BUFFERS], w_codes[g], w_scales[g], c0, n) for c0, n in W_RANGES])
 
-        def chunk_interleave(c):
-            raw, codes, scales, c0, n = chunks[c]
-            interleave("g", op_st[c % 2][:, 0:n * PACK], raw[:, :, c0:c0 + n])
+        def interleave_range(i):
+            raw, codes, scales, c0, n = ranges[i]
+            nc.gpsimd.tensor_scalar(out=side_by_side[i % 2][:, 0:n * PACK].rearrange("p (c j) -> p c j", j=PACK),
+                                    in0=raw[:, :, c0:c0 + n].rearrange("p j c -> p c j"),
+                                    scalar1=1.0, scalar2=0.0, op0=ALU.mult, op1=ALU.add)
 
-        def chunk_quant(c):
-            raw, codes, scales, c0, n = chunks[c]
+        def quantise_range(i):
+            raw, codes, scales, c0, n = ranges[i]
             nc.vector.quantize_mx(out=codes[:, c0:c0 + n].bitcast(E4M3X4), scales=scales[:, c0:c0 + n],
-                                  in_=op_st[c % 2][:, 0:n * PACK])
+                                  in_=side_by_side[i % 2][:, 0:n * PACK])
 
-        def gt_of(h):
-            return (o_banks[0] if h == 1 else gt_bank)[:].bitcast(BF16)
+        def turned_g(h):
+            return (dx_banks[0] if h == 1 else gt_bank)[:].bitcast(BF16)
 
-        def transpose_g(h):
-            dst = gt_of(h)
+        def turn_g(h):
             for j in range(PACK):
-                nc.tensor.transpose(dst[:, j * P:(j + 1) * P], g_of[h][:, j * D:(j + 1) * D], ident16[:])
+                nc.tensor.transpose(turned_g(h)[:, j * P:(j + 1) * P], g_of[h][:, j * D:(j + 1) * D], ident16[:])
 
         def rope_terms(h):
-            gt = gt_of(h)[:, 0:S].unsqueeze(1).to_broadcast([P, 2, S])
-            nc.vector.tensor_tensor(out=terms[h % 2][:], in0=gt, in1=tabs[source(h)[0]][:], op=ALU.mult)
+            both = turned_g(h)[:, 0:S].unsqueeze(1).to_broadcast([P, 2, S])
+            nc.vector.tensor_tensor(out=terms[h % 2][:], in0=both, in1=tables[source(h)[0]][:], op=ALU.mult)
 
-        def sum_terms(h):
+        def add_terms(h):
             halves = du_banks[h % 2][:].rearrange("p (j a b) -> p j a b", j=PACK, a=2)
             ident = ident32[:].rearrange("p (a b) -> p a b", a=2)
             for j in range(PACK):
@@ -165,117 +158,118 @@ def tile_refattention_pa_v_kernel(
                 nc.tensor.matmul(out=halves[:, j, ::-1, :], lhsT=terms[h % 2][:, 1, tok], rhs=ident,
                                  start=False, stop=True, is_transpose=True)
 
+        def square_sums(h):
+            for j in reversed(range(PACK)):
+                nc.scalar.activation(out=squares[:, j, :], in_=z_of[h][:, j, :], func=ACT.Square,
+                                     accum_out=sum_sq[:, h, j:j + 1])
+
+        def make_den(heads):
+            nc.scalar.activation(out=neg_den[:, heads, :], in_=sum_sq[:, heads, :], func=ACT.Copy,
+                                 scale=-1.0, bias=-D * EPS)
+
+        def make_n(heads):
+            nc.vector.reciprocal(out=n_stat[:, heads, :], in_=neg_den[:, heads, :])
+
+        def make_r(heads):
+            nc.scalar.activation(out=r_stat[:, heads, :], in_=n_stat[:, heads, :], func=ACT.Sqrt, scale=-float(D))
+
         def du_of(h, j):
             if h < ROPE_HEADS:
                 return du_banks[h % 2][:, j * D:(j + 1) * D]
             return g_of[h][:, j * D:(j + 1) * D]
 
-        def dot(h, j, slot):
-            nc.vector.scalar_tensor_tensor(out=prod[:, slot, :], in0=du_of(h, j), scalar=nr2[:, h, j:j + 1], in1=z_of[h][:, j, :],
-                                           op0=ALU.mult, op1=ALU.mult, accum_out=cc[:, h, j:j + 1])
+        def make_c(cells):
+            for i, (h, j) in enumerate(cells):
+                nc.vector.scalar_tensor_tensor(out=products[:, i, :], in0=du_of(h, j), scalar=n_stat[:, h, j:j + 1],
+                                               in1=z_of[h][:, j, :], op0=ALU.mult, op1=ALU.mult,
+                                               accum_out=c_stat[:, h, j:j + 1])
 
-        def project(h, j, u):
-            nc.vector.scalar_tensor_tensor(out=u, in0=z_of[h][:, j, :], scalar=cc[:, h, j:j + 1], in1=du_of(h, j),
-                                           op0=ALU.mult, op1=ALU.add)
+        def project(cells, u):
+            for i, (h, j) in reversed(list(enumerate(cells))):
+                nc.vector.scalar_tensor_tensor(out=u[:, i, :], in0=z_of[h][:, j, :], scalar=c_stat[:, h, j:j + 1],
+                                               in1=du_of(h, j), op0=ALU.mult, op1=ALU.add)
 
-        def round_dz(h, j, u):
+        def round_dz(cells, u):
+            for i, (h, j) in enumerate(cells):
+                g, hh = divmod(h, GROUP)
+                nc.scalar.activation(out=dz[g % 2][:, j, hh * D:(hh + 1) * D], in_=u[:, i, :], func=ACT.Copy,
+                                     scale=r_stat[:, h, j:j + 1])
+
+        def head_cells(h):
+            return [(h, j) for j in range(PACK)]
+
+        stored = []
+
+        def store(src_banks, dst, second_half):
+            result = results[len(stored) % OUT_BUFFERS]
+            stored.append(dst)
+            second_half(out=result[:, NT:HID], in_=src_banks[1][:])
+            nc.scalar.copy(out=result[:, 0:NT], in_=src_banks[0][:])
+            nc.sync.dma_start(out=dst, in_=result[:])
+
+        def interleave_dz(h, copy):
             g, hh = divmod(h, GROUP)
-            nc.scalar.activation(out=dz[g % 2][:, j, hh * D:(hh + 1) * D], in_=u, func=ACT.Copy,
-                                 scale=rr[:, h, j:j + 1])
+            copy(out=dz_tok[h % 2][:].rearrange("p (c i j) -> p c j i", i=PACK, j=PACK),
+                 in_=dz[g % 2][:, :, hh * D:(hh + 1) * D].rearrange("p j (c i) -> p c j i", i=PACK))
 
-        def copy_dz_tok(h, engine):
-            g, hh = divmod(h, GROUP)
-            interleave(engine, dz_tok[h % 2][:], dz[g % 2][:, :, hh * D:(hh + 1) * D])
-
-        def tok_quant(h):
-            nc.vector.quantize_mx(out=tok_codes[h % 2][:].bitcast(E5M2X4), scales=tok_sc[h % 2][:],
+        def quantise_tokens(h):
+            nc.vector.quantize_mx(out=tok_codes[h % 2][:].bitcast(E5M2X4), scales=tok_scales[h % 2][:],
                                   in_=dz_tok[h % 2][:])
 
-        def dw_pair(h):
+        def dw_banks_of(h):
             return du_banks if h == HEADS - 1 else dw_banks
 
         def dw_matmuls(h):
             for half in range(2):
                 cols = slice(half * NT, (half + 1) * NT)
-                nc.tensor.matmul_mx(out=dw_pair(h)[half][:], lhsT=tok_codes[h % 2][:].bitcast(E5M2X4),
-                                    lhsT_scale=tok_sc[h % 2][:], rhs=x_codes[:, cols].bitcast(E4M3X4),
-                                    rhs_scale=x_sc[:, cols], start=True, stop=True)
+                nc.tensor.matmul_mx(out=dw_banks_of(h)[half][:], lhsT=tok_codes[h % 2][:].bitcast(E5M2X4),
+                                    lhsT_scale=tok_scales[h % 2][:], rhs=x_codes[:, cols].bitcast(E4M3X4),
+                                    rhs_scale=x_scales[:, cols], start=True, stop=True)
 
-        stores = []
-
-        def evict(src_banks, dst, vector_half):
-            st = stage[len(stores) % STAGE_RING]
-            stores.append(dst)
-            if vector_half:
-                nc.vector.tensor_copy(out=st[:, NT:HID], in_=src_banks[1][:])
-            else:
-                nc.scalar.copy(out=st[:, NT:HID], in_=src_banks[1][:])
-            nc.scalar.copy(out=st[:, 0:NT], in_=src_banks[0][:])
-            nc.sync.dma_start(out=dst, in_=st[:])
-
-        def dw_out(h, vector_half=False):
+        def store_dw(h, second_half):
             kind, hh = source(h)
-            evict(dw_pair(h), (out_1, out_2, out_3)[kind][hh * D:(hh + 1) * D, :], vector_half)
+            store(dw_banks_of(h), (out_1, out_2, out_3)[kind][hh * D:(hh + 1) * D, :], second_half)
 
-        def square_sum(h):
-            for j in reversed(range(PACK)):
-                nc.scalar.activation(out=junk[:, j, :], in_=z_of[h][:, j, :], func=ACT.Square,
-                                     accum_out=ss[:, h, j:j + 1])
+        def words_bank(g):
+            return word_bank if g < K_PASS else du_banks[1]
 
-        def stat_den(m):
-            nc.scalar.activation(out=nden[:, m, :], in_=ss[:, m, :], func=ACT.Copy,
-                                 scale=-1.0, bias=-D * EPS)
-
-        def stat_recip(m):
-            nc.vector.reciprocal(out=nr2[:, m, :], in_=nden[:, m, :])
-
-        def stat_root(m):
-            nc.scalar.activation(out=rr[:, m, :], in_=nr2[:, m, :], func=ACT.Sqrt,
-                                 scale=-float(D))
-
-        def word_bank(g):
-            return wt_bank if g < ROPE_HEADS // GROUP - 1 else du_banks[1]
-
-        def word_transposes(g, js):
-            dst = word_bank(g)[:].rearrange("p (i u t) -> p i u t", u=2, t=P)
-            for i, j in enumerate(js):
+        def turn_words(g, slots):
+            dst = words_bank(g)[:].rearrange("p (i u t) -> p i u t", u=2, t=P)
+            for i, j in enumerate(slots):
                 words = dz[g % 2][:, j, :].bitcast(F32)
                 for u in range(2):
                     nc.tensor.transpose(dst[:, i, u, :], words[:, u::2], ident32[:])
 
-        def word_evict(g, js):
-            n = len(js)
-            src = word_bank(g)[:, 0:n * 2 * P].rearrange("p (i u t) -> p i t u", u=2, t=P)
-            dst = dz_feat[:, js[0] * 2 * P:(js[0] + n) * 2 * P].rearrange("p (i t u) -> p i t u", u=2, t=P)
-            nc.scalar.copy(out=dst, in_=src)
+        def feat_words(slots):
+            return dz_feat[:, slots[0] * 2 * P:(slots[-1] + 1) * 2 * P]
 
-        def feat_quant(g, js):
-            n = len(js)
-            cols = slice(js[0] * P, (js[0] + n) * P)
-            nc.vector.quantize_mx(out=feat_codes[g][:, cols].bitcast(E5M2X4), scales=feat_sc[g][:, cols],
-                                  in_=dz_feat[:, js[0] * 2 * P:(js[0] + n) * 2 * P].bitcast(BF16))
+        def copy_words(g, slots):
+            src = words_bank(g)[:, 0:len(slots) * 2 * P].rearrange("p (i u t) -> p i t u", u=2, t=P)
+            nc.scalar.copy(out=feat_words(slots).rearrange("p (i t u) -> p i t u", u=2, t=P), in_=src)
 
-        dx_bank = {(0, 0): o_banks[0], (0, 1): o_banks[1], (1, 0): gt_bank, (1, 1): du_banks[0],
-                   (2, 0): wt_bank, (2, 1): o_banks[0], (3, 0): o_banks[1], (3, 1): gt_bank}
+        def quantise_features(g, slots):
+            cols = slice(slots[0] * P, (slots[-1] + 1) * P)
+            nc.vector.quantize_mx(out=feat_codes[g][:, cols].bitcast(E5M2X4), scales=feat_scales[g][:, cols],
+                                  in_=feat_words(slots).bitcast(BF16))
 
         def dx_matmul(j, half, g):
             tok = slice(j * P, (j + 1) * P)
             cols = slice(half * NT, (half + 1) * NT)
-            nc.tensor.matmul_mx(out=dx_bank[(j, half)][:], lhsT=feat_codes[g][:, tok].bitcast(E5M2X4),
-                                lhsT_scale=feat_sc[g][:, tok], rhs=w_codes[g][:, cols].bitcast(E4M3X4),
-                                rhs_scale=w_sc[g][:, cols], start=(g == 0), stop=(g == PASSES - 1))
+            nc.tensor.matmul_mx(out=dx_bank_of[(j, half)][:], lhsT=feat_codes[g][:, tok].bitcast(E5M2X4),
+                                lhsT_scale=feat_scales[g][:, tok], rhs=w_codes[g][:, cols].bitcast(E4M3X4),
+                                rhs_scale=w_scales[g][:, cols], start=(g == 0), stop=(g == V_PASS))
 
-        def dx_out(j, vector_half):
+        def store_dx(j):
             dst = out_0.rearrange("b (p j) c -> p (b j) c", j=PACK)[:, j, :]
-            evict([dx_bank[(j, 0)], dx_bank[(j, 1)]], dst, vector_half)
+            store([dx_bank_of[(j, 0)], dx_bank_of[(j, 1)]], dst, nc.vector.tensor_copy)
 
         with tc.manual_schedule():
-            nc.vector.memset(wrows[:, 0, :], 0.0)
+            nc.vector.memset(gain_rows[:, 0, :], 0.0)
             make_identity(nc, ident16[:])
             make_identity(nc, ident32[:])
-            for i, (tab, w) in enumerate(((cos, q_norm_w), (sin, k_norm_w))):
-                nc.sync.dma_start(out=cs_raw[i][:], in_=tab.rearrange("b (p j) d -> p (b j) d", j=PACK))
-                nc.sync.dma_start(out=wrows[i:i + 1, 0, :], in_=w.rearrange("(o d) -> o d", o=1))
+            for i, (trig, gain) in enumerate(((cos, q_norm_w), (sin, k_norm_w))):
+                nc.sync.dma_start(out=trig_raw[i][:], in_=trig.rearrange("b (p j) d -> p (b j) d", j=PACK))
+                nc.sync.dma_start(out=gain_rows[i:i + 1, 0, :], in_=gain.rearrange("(o d) -> o d", o=1))
             load_g(spans[0])
             load_z(spans[0])
             nc.sync.dma_start(out=x_raw[:], in_=hidden_states.rearrange("b (p j) c -> p (b j) c", j=PACK))
@@ -285,170 +279,160 @@ def tile_refattention_pa_v_kernel(
             load_z(spans[2])
             load_g(spans[2])
             later_loads = []
-            for g in range(1, PASSES):
-                if g + 1 < PASSES:
-                    later_loads.append((load_z, spans[g + 2]))
-                later_loads.append((load_w, g))
-                if g + 1 < PASSES:
-                    later_loads.append((load_g, spans[g + 2]))
+            for g in range(1, V_PASS):
+                later_loads.extend([(load_z, spans[g + 2]), (load_w, g), (load_g, spans[g + 2])])
+            later_loads.append((load_w, V_PASS))
 
-            nc.vector.tensor_scalar(out=wrows[:, 1, 0:HALF], in0=wrows[:, 0, HALF:D], scalar1=-1.0, scalar2=None,
-                                    op0=ALU.mult)
-            nc.vector.tensor_copy(out=wrows[:, 1, HALF:D], in_=wrows[:, 0, 0:HALF])
-            wt16 = wt_bank[:].bitcast(BF16)[:, 0:2 * P].rearrange("p (i t) -> p i t", i=2)
+            nc.vector.tensor_scalar(out=gain_rows[:, 1, 0:HALF], in0=gain_rows[:, 0, HALF:D], scalar1=-1.0,
+                                    scalar2=None, op0=ALU.mult)
+            nc.vector.tensor_copy(out=gain_rows[:, 1, HALF:D], in_=gain_rows[:, 0, 0:HALF])
+            turned_trig = [dw_banks[i][:].bitcast(BF16)[:, 0:S] for i in range(2)]
+            turned_gain = word_bank[:].bitcast(BF16)[:, 0:2 * P].rearrange("p (i t) -> p i t", i=2)
             for i in range(2):
-                dst = dw_banks[i][:].bitcast(BF16)
                 for j in range(PACK):
-                    nc.tensor.transpose(dst[:, j * P:(j + 1) * P], cs_raw[i][:, j, :], ident16[:])
-                if i == 0:
-                    for k in range(2):
-                        nc.tensor.transpose(wt16[:, k, :], wrows[:, k, :], ident16[:])
-            transpose_g(0)
-            nc.vector.tensor_copy(out=wcol[:], in_=wt16[:, :, 0:2])
-            cos_t = dw_banks[0][:].bitcast(BF16)[:, 0:S]
-            sin_t = dw_banks[1][:].bitcast(BF16)[:, 0:S]
-            nc.vector.tensor_scalar(out=tabs[0][:, 0, :], in0=cos_t, scalar1=wcol[:, 0, 0:1], scalar2=None, op0=ALU.mult)
-            nc.scalar.activation(out=tabs[0][:, 1, :], in_=sin_t, func=ACT.Copy, scale=wcol[:, 1, 0:1])
-            transpose_g(1)
-            rope_terms(0)
-            sum_terms(0)
-            rope_terms(1)
-            square_sum(0)
-            square_sum(1)
-            nc.scalar.activation(out=tabs[1][:, 0, :], in_=cos_t, func=ACT.Copy, scale=wcol[:, 0, 1:2])
-            stat_den(span_ending[1])
-            stat_recip(span_ending[1])
-            nc.scalar.activation(out=tabs[1][:, 1, :], in_=sin_t, func=ACT.Copy, scale=wcol[:, 1, 1:2])
-            stat_root(span_ending[1])
-            chunk_interleave(0)
-            chunk_interleave(1)
-            square_sum(2)
+                    nc.tensor.transpose(turned_trig[i][:, j * P:(j + 1) * P], trig_raw[i][:, j, :], ident16[:])
+            for i in range(2):
+                nc.tensor.transpose(turned_gain[:, i, :], gain_rows[:, i, :], ident16[:])
+            turn_g(0)
+            nc.vector.tensor_copy(out=gain_cols[:], in_=turned_gain[:, :, 0:2])
 
-            next_ss = SS_LEAD
+            def table_on_scalar(kind, i):
+                nc.scalar.activation(out=tables[kind][:, i, :], in_=turned_trig[i], func=ACT.Copy,
+                                     scale=gain_cols[:, i, kind:kind + 1])
+
+            nc.vector.tensor_scalar(out=tables[0][:, 0, :], in0=turned_trig[0], scalar1=gain_cols[:, 0, 0:1],
+                                    scalar2=None, op0=ALU.mult)
+            table_on_scalar(0, 1)
+            turn_g(1)
+            rope_terms(0)
+            add_terms(0)
+            rope_terms(1)
+            first_span = span_ending[1]
+            square_sums(0)
+            square_sums(1)
+            table_on_scalar(1, 0)
+            make_den(first_span)
+            make_n(first_span)
+            table_on_scalar(1, 1)
+            make_r(first_span)
+            interleave_range(0)
+            interleave_range(1)
+            square_sums(2)
+
+            next_square = SQUARES_AHEAD
             den_due = {}
-            recip_due = {}
-            root_due = {}
             for s in range(ROPE_HEADS):
-                vector_copy = s % GROUP in VECTOR_COPY_PHASES
+                phase = s % GROUP
+                done_pass = s // GROUP - 1
+                rotating = s + 2 < ROPE_HEADS
                 if s >= 1:
-                    for j in range(PACK):
-                        round_dz(s - 1, j, u_t[(s - 1) % 2][:, j, :])
-                if s >= 2:
-                    chunk_interleave(s)
+                    round_dz(head_cells(s - 1), unscaled[(s - 1) % 2])
+                if s >= len(X_RANGES):
+                    interleave_range(s)
                 if s in den_due:
-                    stat_den(den_due[s])
-                if s in root_due:
-                    stat_root(root_due[s])
-                if s + 2 < ROPE_HEADS:
-                    transpose_g(s + 2)
-                if s >= 3:
-                    dw_matmuls(s - 3)
-                if s >= 7 and s % GROUP == 3:
+                    make_den(den_due[s])
+                if s - 1 in den_due:
+                    make_r(den_due[s - 1])
+                if rotating:
+                    turn_g(s + 2)
+                if s >= DW_LAG:
+                    dw_matmuls(s - DW_LAG)
+                if s >= DX_FIRST_STEP and (s - DX_FIRST_STEP) % GROUP == 0:
                     for half in range(2):
-                        dx_matmul(0, half, (s - 7) // GROUP)
+                        dx_matmul(0, half, (s - DX_FIRST_STEP) // GROUP)
                 if s + 1 < ROPE_HEADS:
-                    sum_terms(s + 1)
+                    add_terms(s + 1)
                 if s == ROPE_HEADS - 2:
-                    for g in range(3):
+                    for g in range(K_PASS - 1):
                         dx_matmul(1, 0, g)
                         dx_matmul(2, 0, g)
                 if s == ROPE_HEADS - 1:
-                    dx_matmul(1, 0, 3)
-                    dx_matmul(2, 0, 3)
-                    for g in range(4):
+                    dx_matmul(1, 0, K_PASS - 1)
+                    dx_matmul(2, 0, K_PASS - 1)
+                    for g in range(K_PASS):
                         dx_matmul(1, 1, g)
-                feat_round = None
-                if s >= GROUP and s % GROUP < 2:
-                    feat_round = (0, 1) if s % GROUP == 0 else (2, 3)
-                    word_transposes(s // GROUP - 1, feat_round)
-                for j in range(PACK):
-                    dot(s, j, j)
-                if s + 2 < ROPE_HEADS:
+                word_slots = (2 * phase, 2 * phase + 1)
+                turning_words = done_pass >= 0 and phase < 2
+                if turning_words:
+                    turn_words(done_pass, word_slots)
+                make_c(head_cells(s))
+                if rotating:
                     rope_terms(s + 2)
                 else:
-                    dw_out(s - 3, True)
+                    store_dw(s - DW_LAG, nc.vector.tensor_copy)
                 if s in den_due:
-                    stat_recip(den_due[s])
-                    root_due[s + 1] = den_due[s]
-                if s >= GROUP and s % GROUP == 2:
-                    feat_quant(s // GROUP - 1, (0, 1, 2, 3))
+                    make_n(den_due[s])
+                if done_pass >= 0 and phase == 2:
+                    quantise_features(done_pass, list(range(PACK)))
                 if s >= 2:
-                    tok_quant(s - 2)
-                if s >= 1 and vector_copy:
-                    copy_dz_tok(s - 1, "v")
+                    quantise_tokens(s - 2)
                 if s >= 1:
-                    chunk_quant(s - 1)
-                for j in reversed(range(PACK)):
-                    project(s, j, u_t[s % 2][:, j, :])
+                    quantise_range(s - 1)
+                project(head_cells(s), unscaled[s % 2])
                 if s < len(later_loads):
-                    later_loads[s][0](later_loads[s][1])
-                if s >= 3 and s + 2 < ROPE_HEADS:
-                    dw_out(s - 3)
-                if s >= 1 and not vector_copy:
-                    copy_dz_tok(s - 1, "s")
-                for rep in range(2 if s in EXTRA_SS_STEPS else 1):
-                    if next_ss < HEADS:
-                        square_sum(next_ss)
-                        if next_ss in span_ending:
-                            den_due[s + 1] = span_ending[next_ss]
-                        next_ss = next_ss + 1
-                if feat_round is not None:
-                    word_evict(s // GROUP - 1, feat_round)
-
+                    load, what = later_loads[s]
+                    load(what)
+                if s >= DW_LAG and rotating:
+                    store_dw(s - DW_LAG, nc.scalar.copy)
+                if s >= 1:
+                    interleave_dz(s - 1, nc.scalar.copy)
+                heads_to_square = 2 if s in DOUBLE_SQUARE_STEPS else 1
+                for h in range(next_square, min(next_square + heads_to_square, HEADS)):
+                    square_sums(h)
+                    if h in span_ending:
+                        den_due[s + 1] = span_ending[h]
+                next_square = next_square + heads_to_square
+                if turning_words:
+                    copy_words(done_pass, word_slots)
 
         last = ROPE_HEADS - 1
-        kg = PASSES - 2
-        vg = PASSES - 1
 
-        def cells(batch, u):
-            for i, (h, j) in enumerate(batch):
-                dot(h, j, i)
-            for i, (h, j) in reversed(list(enumerate(batch))):
-                project(h, j, u[:, i, :])
-            for i, (h, j) in enumerate(batch):
-                round_dz(h, j, u[:, i, :])
+        def v_cells(cells, u):
+            make_c(cells)
+            project(cells, u)
+            round_dz(cells, u)
 
-        def feature_road(g, js):
-            word_transposes(g, js)
-            word_evict(g, js)
-            feat_quant(g, js)
+        def feature_road(g, slots):
+            turn_words(g, slots)
+            copy_words(g, slots)
+            quantise_features(g, slots)
 
-        def token_road(h, vector_half):
-            copy_dz_tok(h, "v")
-            tok_quant(h)
+        def token_road(h, second_half):
+            interleave_dz(h, nc.vector.tensor_copy)
+            quantise_tokens(h)
             dw_matmuls(h)
-            dw_out(h, vector_half)
+            store_dw(h, second_half)
 
         dw_matmuls(last - 2)
-        stat_root(root_due[ROPE_HEADS])
-        for j in range(PACK):
-            round_dz(last, j, u_t[last % 2][:, j, :])
-        dw_out(last - 2, False)
-        feature_road(kg, (0, 1))
+        make_r(den_due[last])
+        round_dz(head_cells(last), unscaled[last % 2])
+        feature_road(K_PASS, (0, 1))
         for j in range(2):
+            v_cells([(h, j) for h in range(ROPE_HEADS, HEADS)], unscaled[j])
+            feature_road(V_PASS, (j,))
+            if j == 0:
+                quantise_range(last)
             for half in range(2):
-                dx_matmul(j, half, kg)
-        for a in range(GROUP):
-            cells([(ROPE_HEADS + hh, a) for hh in range(a, GROUP)], u_t[0])
-            if a == 0:
-                chunk_quant(last)
-                tok_quant(last - 1)
+                for g in (K_PASS, V_PASS):
+                    dx_matmul(j, half, g)
+            if j == 0:
+                store_dw(last - 2, nc.scalar.copy)
+            store_dx(j)
+            if j == 0:
+                quantise_tokens(last - 1)
                 dw_matmuls(last - 1)
-                dw_out(last - 1, False)
-            feature_road(vg, (a,))
+                store_dw(last - 1, nc.scalar.copy)
+                token_road(last, nc.scalar.copy)
+        feature_road(K_PASS, (2, 3))
+        for h in range(ROPE_HEADS, HEADS):
+            v_cells([(h, j) for j in (2, 3)], unscaled[h % 2])
+            if h + 1 < HEADS:
+                token_road(h, nc.vector.tensor_copy)
+        feature_road(V_PASS, (2, 3))
+        token_road(HEADS - 1, nc.vector.tensor_copy)
+        for j in (2, 3):
             for half in range(2):
-                dx_matmul(a, half, vg)
-            dx_out(a, a >= 0)
-            if a == 0:
-                token_road(last, False)
-                for g in range(vg):
-                    if g == kg:
-                        feature_road(kg, (2, 3))
-                        dx_matmul(2, 0, kg)
-                    dx_matmul(2, 1, g)
-                    dx_matmul(3, 0, g)
-            if a == 1:
-                for g in range(vg):
-                    dx_matmul(3, 1, g)
-            cells([(ROPE_HEADS + a, j) for j in range(a + 1, PACK)], u_t[1])
-            token_road(ROPE_HEADS + a, a >= 1)
+                first = K_PASS if (j, half) == (2, 0) else 0
+                for g in range(first, PASSES):
+                    dx_matmul(j, half, g)
+            store_dx(j)

from contextlib import ExitStack

import concourse.mybir as mybir
from concourse.masks import make_identity

F32 = mybir.dt.float32
BF16 = mybir.dt.bfloat16
U32 = mybir.dt.uint32
U8 = mybir.dt.uint8
E4M3X4 = mybir.dt.float8_e4m3fn_x4
E5M2X4 = mybir.dt.float8_e5m2_x4
ALU = mybir.AluOpType
ACT = mybir.ActivationFunctionType

P = 128
S = 512
HID = 1024
D = 128
HALF = D // 2
PACK = 4
EPS = 1e-6
Q_HEADS = 16
ROPE_HEADS = 20
HEADS = 24
GROUP = 4
PASSES = HEADS // GROUP
K_PASS = PASSES - 2
V_PASS = PASSES - 1
NT = 512
FLOPS = 2 * 2 * S * HEADS * D * HID

X_RANGES = ((0, 512), (512, 512))
W_RANGES = ((0, 384), (384, 384), (768, 256))
W_BUFFERS = 3
OUT_BUFFERS = 7
SQUARES_AHEAD = 3
DOUBLE_SQUARE_STEPS = (1, 2)
DW_LAG = 3
DX_FIRST_STEP = 7


def tile_refattention_pa_v_kernel(
    tc, hidden_states, cos, sin, Wq, Wk, Wv, q_norm_w, k_norm_w, q_pre, k_pre, v_pre,
    grad_0, grad_1, grad_2, out_0, out_1, out_2, out_3,
):
    nc = tc.nc
    with ExitStack() as ctx:
        sb = ctx.enter_context(tc.tile_pool(name="sb", bufs=1))
        ps = ctx.enter_context(tc.psum_pool(name="ps", bufs=1))

        def sbt(name, shape, dtype):
            return sb.tile(shape, dtype, name=name, align_bytes=64)

        banks = [ps.tile([P, NT], F32, name="bank%d" % b) for b in range(8)]
        gt_bank, du_banks, dw_banks, word_bank, dx_banks = banks[0], banks[1:3], banks[3:5], banks[5], banks[6:8]
        dx_bank_of = {(0, 0): dx_banks[0], (0, 1): dx_banks[1], (1, 0): gt_bank, (1, 1): du_banks[0],
                      (2, 0): word_bank, (2, 1): dx_banks[0], (3, 0): dx_banks[1], (3, 1): gt_bank}

        ident32 = sbt("ident32", [P, P], F32)
        ident16 = sbt("ident16", [P, P], BF16)
        trig_raw = [sbt("trig_raw%d" % i, [P, PACK, D], BF16) for i in range(2)]
        gain_rows = sbt("gain_rows", [P, 2, D], BF16)
        gain_cols = sbt("gain_cols", [P, 2, 2], F32)
        tables = [sbt("table%d" % i, [P, 2, S], F32) for i in range(2)]
        x_raw = sbt("x_raw", [P, PACK, HID], BF16)
        x_codes = sbt("x_codes", [P, HID], U32)
        x_scales = sbt("x_scales", [P, HID], U8)
        w_raw = [sbt("w_raw%d" % i, [P, PACK, HID], BF16) for i in range(W_BUFFERS)]
        side_by_side = [sbt("side_by_side%d" % i, [P, NT * PACK], BF16) for i in range(2)]
        w_codes = [sbt("w_codes%d" % i, [P, HID], U32) for i in range(PASSES)]
        w_scales = [sbt("w_scales%d" % i, [P, HID], U8) for i in range(PASSES)]
        terms = [sbt("terms%d" % i, [P, 2, S], F32) for i in range(2)]
        unscaled = [sbt("unscaled%d" % i, [P, PACK, D], F32) for i in range(2)]
        products = sbt("products", [P, PACK, D], BF16)
        squares = sbt("squares", [P, PACK, D], BF16)
        dz = [sbt("dz%d" % i, [P, PACK, GROUP * D], BF16) for i in range(2)]
        dz_tok = [sbt("dz_tok%d" % i, [P, D * PACK], BF16) for i in range(2)]
        tok_codes = [sbt("tok_codes%d" % i, [P, D], U32) for i in range(2)]
        tok_scales = [sbt("tok_scales%d" % i, [P, D], U8) for i in range(2)]
        dz_feat = sbt("dz_feat", [P, S * 2], F32)
        feat_codes = [sbt("feat_codes%d" % i, [P, S], U32) for i in range(PASSES)]
        feat_scales = [sbt("feat_scales%d" % i, [P, S], U8) for i in range(PASSES)]
        results = [sbt("result%d" % i, [P, HID], F32) for i in range(OUT_BUFFERS)]
        sum_sq = sbt("sum_sq", [P, HEADS, PACK], F32)
        neg_den = sbt("neg_den", [P, HEADS, PACK], F32)
        n_stat = sbt("n_stat", [P, HEADS, PACK], F32)
        r_stat = sbt("r_stat", [P, HEADS, PACK], F32)
        c_stat = sbt("c_stat", [P, HEADS, PACK], F32)

        spans = [(0, 2), (2, 2)] + [(h0, GROUP) for h0 in range(GROUP, HEADS, GROUP)]
        span_ending = {h0 + n - 1: slice(h0, h0 + n) for h0, n in spans}
        g_of = {}
        z_of = {}

        def source(h):
            if h < Q_HEADS:
                return 0, h
            if h < ROPE_HEADS:
                return 1, h - Q_HEADS
            return 2, h - ROPE_HEADS

        def load_g(span):
            h0, n = span
            kind, hh = source(h0)
            src = (grad_0, grad_1, grad_2)[kind].rearrange("b h (p j) d -> p (b h) (j d)", j=PACK)
            loaded = sbt("g%d" % h0, [P, n, PACK * D], BF16)
            nc.sync.dma_start(out=loaded[:], in_=src[:, hh:hh + n, :])
            for i in range(n):
                g_of[h0 + i] = loaded[:, i, :]

        def load_z(span):
            h0, n = span
            kind, hh = source(h0)
            src = (q_pre, k_pre, v_pre)[kind].rearrange("b (p j) f -> p (b j) f", j=PACK)
            loaded = sbt("z%d" % h0, [P, PACK, n * D], F32)
            nc.sync.dma_start(out=loaded[:], in_=src[:, :, hh * D:(hh + n) * D])
            for i in range(n):
                z_of[h0 + i] = loaded[:, :, i * D:(i + 1) * D]

        def load_w(g):
            kind, hh = source(g * GROUP)
            src = (Wq, Wk, Wv)[kind][hh * D:(hh + GROUP) * D, :].rearrange("(p j) c -> p j c", j=PACK)
            nc.sync.dma_start(out=w_raw[g % W_BUFFERS][:], in_=src)

        ranges = [(x_raw, x_codes, x_scales, c0, n) for c0, n in X_RANGES]
        for g in range(PASSES):
            ranges.extend([(w_raw[g % W_BUFFERS], w_codes[g], w_scales[g], c0, n) for c0, n in W_RANGES])

        def interleave_range(i):
            raw, codes, scales, c0, n = ranges[i]
            nc.gpsimd.tensor_scalar(out=side_by_side[i % 2][:, 0:n * PACK].rearrange("p (c j) -> p c j", j=PACK),
                                    in0=raw[:, :, c0:c0 + n].rearrange("p j c -> p c j"),
                                    scalar1=1.0, scalar2=0.0, op0=ALU.mult, op1=ALU.add)

        def quantise_range(i):
            raw, codes, scales, c0, n = ranges[i]
            nc.vector.quantize_mx(out=codes[:, c0:c0 + n].bitcast(E4M3X4), scales=scales[:, c0:c0 + n],
                                  in_=side_by_side[i % 2][:, 0:n * PACK])

        def turned_g(h):
            return (dx_banks[0] if h == 1 else gt_bank)[:].bitcast(BF16)

        def turn_g(h):
            for j in range(PACK):
                nc.tensor.transpose(turned_g(h)[:, j * P:(j + 1) * P], g_of[h][:, j * D:(j + 1) * D], ident16[:])

        def rope_terms(h):
            both = turned_g(h)[:, 0:S].unsqueeze(1).to_broadcast([P, 2, S])
            nc.vector.tensor_tensor(out=terms[h % 2][:], in0=both, in1=tables[source(h)[0]][:], op=ALU.mult)

        def add_terms(h):
            halves = du_banks[h % 2][:].rearrange("p (j a b) -> p j a b", j=PACK, a=2)
            ident = ident32[:].rearrange("p (a b) -> p a b", a=2)
            for j in range(PACK):
                tok = slice(j * P, (j + 1) * P)
                nc.tensor.matmul(out=halves[:, j, :, :], lhsT=terms[h % 2][:, 0, tok], rhs=ident,
                                 start=True, stop=False, is_transpose=True)
                nc.tensor.matmul(out=halves[:, j, ::-1, :], lhsT=terms[h % 2][:, 1, tok], rhs=ident,
                                 start=False, stop=True, is_transpose=True)

        def square_sums(h):
            for j in reversed(range(PACK)):
                nc.scalar.activation(out=squares[:, j, :], in_=z_of[h][:, j, :], func=ACT.Square,
                                     accum_out=sum_sq[:, h, j:j + 1])

        def make_den(heads):
            nc.scalar.activation(out=neg_den[:, heads, :], in_=sum_sq[:, heads, :], func=ACT.Copy,
                                 scale=-1.0, bias=-D * EPS)

        def make_n(heads):
            nc.vector.reciprocal(out=n_stat[:, heads, :], in_=neg_den[:, heads, :])

        def make_r(heads):
            nc.scalar.activation(out=r_stat[:, heads, :], in_=n_stat[:, heads, :], func=ACT.Sqrt, scale=-float(D))

        def du_of(h, j):
            if h < ROPE_HEADS:
                return du_banks[h % 2][:, j * D:(j + 1) * D]
            return g_of[h][:, j * D:(j + 1) * D]

        def make_c(cells):
            for i, (h, j) in enumerate(cells):
                nc.vector.scalar_tensor_tensor(out=products[:, i, :], in0=du_of(h, j), scalar=n_stat[:, h, j:j + 1],
                                               in1=z_of[h][:, j, :], op0=ALU.mult, op1=ALU.mult,
                                               accum_out=c_stat[:, h, j:j + 1])

        def project(cells, u):
            for i, (h, j) in reversed(list(enumerate(cells))):
                nc.vector.scalar_tensor_tensor(out=u[:, i, :], in0=z_of[h][:, j, :], scalar=c_stat[:, h, j:j + 1],
                                               in1=du_of(h, j), op0=ALU.mult, op1=ALU.add)

        def round_dz(cells, u):
            for i, (h, j) in enumerate(cells):
                g, hh = divmod(h, GROUP)
                nc.scalar.activation(out=dz[g % 2][:, j, hh * D:(hh + 1) * D], in_=u[:, i, :], func=ACT.Copy,
                                     scale=r_stat[:, h, j:j + 1])

        def head_cells(h):
            return [(h, j) for j in range(PACK)]

        stored = []

        def store(src_banks, dst, second_half):
            result = results[len(stored) % OUT_BUFFERS]
            stored.append(dst)
            second_half(out=result[:, NT:HID], in_=src_banks[1][:])
            nc.scalar.copy(out=result[:, 0:NT], in_=src_banks[0][:])
            nc.sync.dma_start(out=dst, in_=result[:])

        def interleave_dz(h, copy):
            g, hh = divmod(h, GROUP)
            copy(out=dz_tok[h % 2][:].rearrange("p (c i j) -> p c j i", i=PACK, j=PACK),
                 in_=dz[g % 2][:, :, hh * D:(hh + 1) * D].rearrange("p j (c i) -> p c j i", i=PACK))

        def quantise_tokens(h):
            nc.vector.quantize_mx(out=tok_codes[h % 2][:].bitcast(E5M2X4), scales=tok_scales[h % 2][:],
                                  in_=dz_tok[h % 2][:])

        def dw_banks_of(h):
            return du_banks if h == HEADS - 1 else dw_banks

        def dw_matmuls(h):
            for half in range(2):
                cols = slice(half * NT, (half + 1) * NT)
                nc.tensor.matmul_mx(out=dw_banks_of(h)[half][:], lhsT=tok_codes[h % 2][:].bitcast(E5M2X4),
                                    lhsT_scale=tok_scales[h % 2][:], rhs=x_codes[:, cols].bitcast(E4M3X4),
                                    rhs_scale=x_scales[:, cols], start=True, stop=True)

        def store_dw(h, second_half):
            kind, hh = source(h)
            store(dw_banks_of(h), (out_1, out_2, out_3)[kind][hh * D:(hh + 1) * D, :], second_half)

        def words_bank(g):
            return word_bank if g < K_PASS else du_banks[1]

        def turn_words(g, slots):
            dst = words_bank(g)[:].rearrange("p (i u t) -> p i u t", u=2, t=P)
            for i, j in enumerate(slots):
                words = dz[g % 2][:, j, :].bitcast(F32)
                for u in range(2):
                    nc.tensor.transpose(dst[:, i, u, :], words[:, u::2], ident32[:])

        def feat_words(slots):
            return dz_feat[:, slots[0] * 2 * P:(slots[-1] + 1) * 2 * P]

        def copy_words(g, slots):
            src = words_bank(g)[:, 0:len(slots) * 2 * P].rearrange("p (i u t) -> p i t u", u=2, t=P)
            nc.scalar.copy(out=feat_words(slots).rearrange("p (i t u) -> p i t u", u=2, t=P), in_=src)

        def quantise_features(g, slots):
            cols = slice(slots[0] * P, (slots[-1] + 1) * P)
            nc.vector.quantize_mx(out=feat_codes[g][:, cols].bitcast(E5M2X4), scales=feat_scales[g][:, cols],
                                  in_=feat_words(slots).bitcast(BF16))

        def dx_matmul(j, half, g):
            tok = slice(j * P, (j + 1) * P)
            cols = slice(half * NT, (half + 1) * NT)
            nc.tensor.matmul_mx(out=dx_bank_of[(j, half)][:], lhsT=feat_codes[g][:, tok].bitcast(E5M2X4),
                                lhsT_scale=feat_scales[g][:, tok], rhs=w_codes[g][:, cols].bitcast(E4M3X4),
                                rhs_scale=w_scales[g][:, cols], start=(g == 0), stop=(g == V_PASS))

        def store_dx(j):
            dst = out_0.rearrange("b (p j) c -> p (b j) c", j=PACK)[:, j, :]
            store([dx_bank_of[(j, 0)], dx_bank_of[(j, 1)]], dst, nc.vector.tensor_copy)

        with tc.manual_schedule():
            nc.vector.memset(gain_rows[:, 0, :], 0.0)
            make_identity(nc, ident16[:])
            make_identity(nc, ident32[:])
            for i, (trig, gain) in enumerate(((cos, q_norm_w), (sin, k_norm_w))):
                nc.sync.dma_start(out=trig_raw[i][:], in_=trig.rearrange("b (p j) d -> p (b j) d", j=PACK))
                nc.sync.dma_start(out=gain_rows[i:i + 1, 0, :], in_=gain.rearrange("(o d) -> o d", o=1))
            load_g(spans[0])
            load_z(spans[0])
            nc.sync.dma_start(out=x_raw[:], in_=hidden_states.rearrange("b (p j) c -> p (b j) c", j=PACK))
            load_g(spans[1])
            load_z(spans[1])
            load_w(0)
            load_z(spans[2])
            load_g(spans[2])
            later_loads = []
            for g in range(1, V_PASS):
                later_loads.extend([(load_z, spans[g + 2]), (load_w, g), (load_g, spans[g + 2])])
            later_loads.append((load_w, V_PASS))

            nc.vector.tensor_scalar(out=gain_rows[:, 1, 0:HALF], in0=gain_rows[:, 0, HALF:D], scalar1=-1.0,
                                    scalar2=None, op0=ALU.mult)
            nc.vector.tensor_copy(out=gain_rows[:, 1, HALF:D], in_=gain_rows[:, 0, 0:HALF])
            turned_trig = [dw_banks[i][:].bitcast(BF16)[:, 0:S] for i in range(2)]
            turned_gain = word_bank[:].bitcast(BF16)[:, 0:2 * P].rearrange("p (i t) -> p i t", i=2)
            for i in range(2):
                for j in range(PACK):
                    nc.tensor.transpose(turned_trig[i][:, j * P:(j + 1) * P], trig_raw[i][:, j, :], ident16[:])
            for i in range(2):
                nc.tensor.transpose(turned_gain[:, i, :], gain_rows[:, i, :], ident16[:])
            turn_g(0)
            nc.vector.tensor_copy(out=gain_cols[:], in_=turned_gain[:, :, 0:2])

            def table_on_scalar(kind, i):
                nc.scalar.activation(out=tables[kind][:, i, :], in_=turned_trig[i], func=ACT.Copy,
                                     scale=gain_cols[:, i, kind:kind + 1])

            nc.vector.tensor_scalar(out=tables[0][:, 0, :], in0=turned_trig[0], scalar1=gain_cols[:, 0, 0:1],
                                    scalar2=None, op0=ALU.mult)
            table_on_scalar(0, 1)
            turn_g(1)
            rope_terms(0)
            add_terms(0)
            rope_terms(1)
            first_span = span_ending[1]
            square_sums(0)
            square_sums(1)
            table_on_scalar(1, 0)
            make_den(first_span)
            make_n(first_span)
            table_on_scalar(1, 1)
            make_r(first_span)
            interleave_range(0)
            interleave_range(1)
            square_sums(2)

            next_square = SQUARES_AHEAD
            den_due = {}
            for s in range(ROPE_HEADS):
                phase = s % GROUP
                done_pass = s // GROUP - 1
                rotating = s + 2 < ROPE_HEADS
                if s >= 1:
                    round_dz(head_cells(s - 1), unscaled[(s - 1) % 2])
                if s >= len(X_RANGES):
                    interleave_range(s)
                if s in den_due:
                    make_den(den_due[s])
                if s - 1 in den_due:
                    make_r(den_due[s - 1])
                if rotating:
                    turn_g(s + 2)
                if s >= DW_LAG:
                    dw_matmuls(s - DW_LAG)
                if s >= DX_FIRST_STEP and (s - DX_FIRST_STEP) % GROUP == 0:
                    for half in range(2):
                        dx_matmul(0, half, (s - DX_FIRST_STEP) // GROUP)
                if s + 1 < ROPE_HEADS:
                    add_terms(s + 1)
                if s == ROPE_HEADS - 2:
                    for g in range(K_PASS - 1):
                        dx_matmul(1, 0, g)
                        dx_matmul(2, 0, g)
                if s == ROPE_HEADS - 1:
                    dx_matmul(1, 0, K_PASS - 1)
                    dx_matmul(2, 0, K_PASS - 1)
                    for g in range(K_PASS):
                        dx_matmul(1, 1, g)
                word_slots = (2 * phase, 2 * phase + 1)
                turning_words = done_pass >= 0 and phase < 2
                if turning_words:
                    turn_words(done_pass, word_slots)
                make_c(head_cells(s))
                if rotating:
                    rope_terms(s + 2)
                else:
                    store_dw(s - DW_LAG, nc.vector.tensor_copy)
                if s in den_due:
                    make_n(den_due[s])
                if done_pass >= 0 and phase == 2:
                    quantise_features(done_pass, list(range(PACK)))
                if s >= 2:
                    quantise_tokens(s - 2)
                if s >= 1:
                    quantise_range(s - 1)
                project(head_cells(s), unscaled[s % 2])
                if s < len(later_loads):
                    load, what = later_loads[s]
                    load(what)
                if s >= DW_LAG and rotating:
                    store_dw(s - DW_LAG, nc.scalar.copy)
                if s >= 1:
                    interleave_dz(s - 1, nc.scalar.copy)
                heads_to_square = 2 if s in DOUBLE_SQUARE_STEPS else 1
                for h in range(next_square, min(next_square + heads_to_square, HEADS)):
                    square_sums(h)
                    if h in span_ending:
                        den_due[s + 1] = span_ending[h]
                next_square = next_square + heads_to_square
                if turning_words:
                    copy_words(done_pass, word_slots)

        last = ROPE_HEADS - 1

        def v_cells(cells, u):
            make_c(cells)
            project(cells, u)
            round_dz(cells, u)

        def feature_road(g, slots):
            turn_words(g, slots)
            copy_words(g, slots)
            quantise_features(g, slots)

        def token_road(h, second_half):
            interleave_dz(h, nc.vector.tensor_copy)
            quantise_tokens(h)
            dw_matmuls(h)
            store_dw(h, second_half)

        dw_matmuls(last - 2)
        make_r(den_due[last])
        round_dz(head_cells(last), unscaled[last % 2])
        feature_road(K_PASS, (0, 1))
        for j in range(2):
            v_cells([(h, j) for h in range(ROPE_HEADS, HEADS)], unscaled[j])
            feature_road(V_PASS, (j,))
            if j == 0:
                quantise_range(last)
            for half in range(2):
                for g in (K_PASS, V_PASS):
                    dx_matmul(j, half, g)
            if j == 0:
                store_dw(last - 2, nc.scalar.copy)
            store_dx(j)
            if j == 0:
                quantise_tokens(last - 1)
                dw_matmuls(last - 1)
                store_dw(last - 1, nc.scalar.copy)
                token_road(last, nc.scalar.copy)
        feature_road(K_PASS, (2, 3))
        for h in range(ROPE_HEADS, HEADS):
            v_cells([(h, j) for j in (2, 3)], unscaled[h % 2])
            if h + 1 < HEADS:
                token_road(h, nc.vector.tensor_copy)
        feature_road(V_PASS, (2, 3))
        token_road(HEADS - 1, nc.vector.tensor_copy)
        for j in (2, 3):
            for half in range(2):
                first = K_PASS if (j, half) == (2, 0) else 0
                for g in range(first, PASSES):
                    dx_matmul(j, half, g)
            store_dx(j)
